import numpy as np
import ml_dtypes


def mxq(x, axis, fmt="e4m3"):
    dtype, down = {"e4m3": (ml_dtypes.float8_e4m3fn, 7), "e5m2": (ml_dtypes.float8_e5m2, 14)}[fmt]
    v = np.moveaxis(np.asarray(x, np.float32).astype(ml_dtypes.bfloat16).astype(np.float64), axis, -1)
    blocks = v.reshape(v.shape[:-1] + (-1, 32))
    amax = np.abs(blocks).max(-1, keepdims=True)
    byte = np.maximum(np.where(amax > 0, np.frexp(amax)[1] - 1 + 127, 0) - down, 1)
    scale = np.exp2(byte - 127.0)
    codes = (blocks / scale).astype(np.float32).astype(dtype).astype(np.float64)
    return np.moveaxis((codes * scale).reshape(v.shape), -1, axis)


WIDE = False


def mx_kscale(k):
    if not WIDE:
        return np.ones(k)
    levels = np.array([10, -10, 5, -5, 0])
    a = np.random.permutation(np.resize(levels, k // 512 * 4)).reshape(k // 512, 4)
    idx = np.arange(k)
    return np.exp2(a[idx // 512, idx % 128 // 32])


BF16 = ml_dtypes.bfloat16


def bf(x):
    return np.asarray(x, np.float32).astype(BF16)


def f64(x):
    return np.asarray(x).astype(np.float64)


E2M1 = np.array([0.0, 0.5, 1.0, 1.5, 2.0, 3.0, 4.0, 6.0, -0.0, -0.5, -1.0, -1.5, -2.0, -3.0, -4.0, -6.0])


def pack_weight(w, fmt):
    k, n = w.shape
    w = f64(bf(w)).reshape(k // 32, 32, n)
    amax = np.abs(w).max(1)
    if fmt == "e4m3":
        byte = np.frexp(amax)[1] - 1 + 127 - 7
    else:
        mant, ex = np.frexp(amax / 6.0)
        byte = np.where(mant > 0.5, ex, ex - 1) + 127
    byte = np.clip(np.where(amax > 0, byte, 1), 1, 254)
    scaled = (w * np.exp2(127.0 - byte)[:, None, :]).reshape(k, n).astype(np.float32)
    by_word = np.ascontiguousarray(scaled.reshape(k // 512, 128, 4, n).transpose(0, 1, 3, 2))
    if fmt == "e4m3":
        words = by_word.astype(ml_dtypes.float8_e4m3fn).view(np.uint8)
    else:
        c = by_word.astype(ml_dtypes.float4_e2m1fn).view(np.uint8) & 0xF
        words = c[..., 0::2] | (c[..., 1::2] << 4)
    return np.ascontiguousarray(words), np.ascontiguousarray(byte.astype(np.uint8).reshape(k // 512, 16, n))


def unpack_weight(words, scales, fmt):
    g, p, n, _ = words.shape
    if fmt == "e4m3":
        vals = np.ascontiguousarray(words).view(ml_dtypes.float8_e4m3fn).astype(np.float64)
    else:
        nib = np.empty((g, p, n, 4), np.uint8)
        nib[..., 0::2] = words & 0xF
        nib[..., 1::2] = words >> 4
        vals = E2M1[nib]
    vals = vals * np.repeat(np.exp2(scales.astype(np.float64) - 127.0), 8, axis=1)[..., None]
    return vals.transpose(0, 1, 3, 2).reshape(g * 512, n)

def pack4(w):
    words, scales = pack_weight(w, "e2m1")
    return words.reshape(words.shape[0], 128, -1), scales


def unpack4(words, scales):
    return unpack_weight(words.reshape(words.shape[0], 128, -1, 2), scales, "e2m1")


N, MI0, MI1, MS, MG, MO0, MO1, DV = 4096, 128, 128, 512, 512, 256, 256, 3
EPS = 1e-5


def irlin_mx(x, mul0, mul1, w0, w1):
    n = x.shape[0]
    x0 = x[:, :mul0]
    x1 = x[:, mul0:].reshape(n, mul1, DV).transpose(0, 2, 1)
    y0 = (mxq(x0, 1, "e4m3") @ w0) * (1.0 / np.sqrt(mul0))
    y1 = (mxq(x1, 2, "e4m3") @ w1).transpose(0, 2, 1) * (1.0 / np.sqrt(mul1))
    return np.concatenate([y0, y1.reshape(n, -1)], axis=-1)


def irlin_plain(x, mul0, mul1, w0, w1):
    n = x.shape[0]
    x0 = x[:, :mul0]
    x1 = x[:, mul0:].reshape(n, mul1, DV).transpose(0, 2, 1)
    y0 = (x0 @ w0) * (1.0 / np.sqrt(mul0))
    y1 = (x1 @ w1).transpose(0, 2, 1) * (1.0 / np.sqrt(mul1))
    return np.concatenate([y0, y1.reshape(n, -1)], axis=-1)


def batchnorm(x, w, b):
    n = x.shape[0]
    s = x[:, :MO0]
    v = x[:, MO0:].reshape(n, MO1, DV)
    s = s - s.mean(0)
    s_inv = 1.0 / np.sqrt((s * s).mean(0) + EPS)
    s = s * (s_inv * w[:MO0]) + b
    v_inv = 1.0 / np.sqrt((v * v).mean(-1).mean(0) + EPS)
    v = v * (v_inv * w[MO0:])[None, :, None]
    return np.concatenate([s, v.reshape(n, -1)], axis=-1)


def setup_inputs():
    s0, s1 = mx_kscale(MS), mx_kscale(MG)
    h0 = (0.1 + 0.3 * np.random.standard_normal((N, MS))) * s0
    h1 = 0.28 * np.random.standard_normal((N, MG, DV)) * s1[None, :, None]
    features = bf(np.random.standard_normal((N, MI0 + DV * MI1)))
    w0_words, w0_scales = pack4(np.random.standard_normal((MS, MO0)) / s0[:, None])
    w1_words, w1_scales = pack4(np.random.standard_normal((MG, MO1)) / s1[:, None])
    return {"h2": bf(np.concatenate([h0, h1.reshape(N, -1)], axis=-1)),
            "features": features,
            "lin3_W0_words": w0_words,
            "lin3_W0_scales": w0_scales,
            "lin3_W1_words": w1_words,
            "lin3_W1_scales": w1_scales,
            "byp_W0": bf(np.random.standard_normal((MI0, MO0))),
            "byp_W1": bf(np.random.standard_normal((MI1, MO1))),
            "bn_weight": bf(1.0 + 0.1 * np.random.standard_normal(MO0 + MO1)),
            "bn_bias": bf(0.1 * np.random.standard_normal(MO0))}


def reference(h2, features, lin3_W0_words, lin3_W0_scales, lin3_W1_words, lin3_W1_scales, byp_W0, byp_W1, bn_weight, bn_bias):
    out = irlin_mx(f64(h2), MS, MG, unpack4(lin3_W0_words, lin3_W0_scales), unpack4(lin3_W1_words, lin3_W1_scales))
    out = out + irlin_plain(f64(features), MI0, MI1, f64(byp_W0), f64(byp_W1))
    return batchnorm(out, f64(bn_weight), f64(bn_bias))

@@ -1,0 +1,326 @@
+import math
+from contextlib import ExitStack
+
+import concourse.mybir as mybir
+from concourse.masks import make_identity
+
+F32 = mybir.dt.float32
+BF16 = mybir.dt.bfloat16
+I32 = mybir.dt.int32
+U32 = mybir.dt.uint32
+U8 = mybir.dt.uint8
+FP8X4 = mybir.dt.float8_e4m3fn_x4
+FP4X4 = mybir.dt.float4_e2m1fn_x4
+ADD = mybir.AluOpType.add
+MULT = mybir.AluOpType.mult
+SQUARE = mybir.ActivationFunctionType.Square
+
+P = 128
+NODES = 4096
+NODE_TILES = NODES // P
+CHUNK_TILES = 4
+CHUNK = CHUNK_TILES * P
+CHUNKS = NODES // CHUNK
+DV = 3
+GROUPS = 1 + DV
+HID = 512
+BYP = 128
+OUT = 256
+HALVES = OUT // P
+BLOCKS = GROUPS * HALVES
+EPS = 1e-5
+
+FLOPS = 2 * NODES * GROUPS * OUT * (HID + BYP)
+
+
+def tile_feedforward_pb_t_kernel(
+    tc,
+    h2,
+    features,
+    lin3_W0_words,
+    lin3_W0_scales,
+    lin3_W1_words,
+    lin3_W1_scales,
+    byp_W0,
+    byp_W1,
+    bn_weight,
+    bn_bias,
+    out,
+):
+    nc = tc.nc
+    h2_tiles = h2.rearrange("(p j) c -> p j c", j=NODE_TILES)
+    features_tiles = features.rearrange("(p j) c -> p j c", j=NODE_TILES)
+    out_tiles = out.rearrange("(p j) c -> p j c", j=NODE_TILES)
+
+    with ExitStack() as whole:
+        keep = whole.enter_context(tc.tile_pool(name="keep", bufs=1))
+
+        y = keep.tile([P, BLOCKS, NODES], F32)
+        scalar_stats = keep.tile([P, HALVES, CHUNKS, 6], F32)
+        vector_squares = keep.tile([P, HALVES, DV, CHUNKS], F32)
+        gain = keep.tile([P, 2 * HALVES], F32)
+        shift = keep.tile([P, HALVES], F32)
+
+        with ExitStack() as first:
+            loads = first.enter_context(tc.tile_pool(name="loads", bufs=2))
+            sorting = first.enter_context(tc.tile_pool(name="sorting", bufs=3))
+            grouping = first.enter_context(tc.tile_pool(name="grouping", bufs=2))
+            operands = first.enter_context(tc.tile_pool(name="operands", bufs=2))
+            sums = first.enter_context(tc.tile_pool(name="sums", bufs=3))
+            scrap = first.enter_context(tc.tile_pool(name="scrap", bufs=1))
+            flip_psum = first.enter_context(tc.psum_pool(name="flip_psum", bufs=3))
+            feat_psum = first.enter_context(tc.psum_pool(name="feat_psum", bufs=1))
+            mx_psum = first.enter_context(tc.psum_pool(name="mx_psum", bufs=2))
+            byp_psum = first.enter_context(tc.psum_pool(name="byp_psum", bufs=2))
+
+            def load_chunk(c):
+                tiles = slice(c * CHUNK_TILES, (c + 1) * CHUNK_TILES)
+                x_scalars = loads.tile([P, CHUNK_TILES, HID], BF16, name="x_scalars")
+                nc.sync.dma_start(out=x_scalars[:], in_=h2_tiles[:, tiles, 0:HID])
+                x_vectors = loads.tile([P, CHUNK_TILES, DV * HID], BF16, name="x_vectors")
+                nc.sync.dma_start(out=x_vectors[:], in_=h2_tiles[:, tiles, HID:])
+                f_rows = loads.tile([P, CHUNK_TILES, GROUPS * BYP], BF16, name="f_rows")
+                nc.sync.dma_start(out=f_rows[:], in_=features_tiles[:, tiles, :])
+                return {"x_scalars": x_scalars, "x_vectors": x_vectors, "f_rows": f_rows}
+
+            loaded = {0: load_chunk(0)}
+
+            ident_f32 = keep.tile([P, P], F32)
+            make_identity(nc, ident_f32[:])
+            ident_bf16 = keep.tile([P, P], BF16)
+            make_identity(nc, ident_bf16[:])
+
+            warm = keep.tile([P, 1], F32)
+            nc.vector.memset(warm[:], 1.0)
+            nc.scalar.sqrt(out=warm[:], in_=warm[:])
+
+            w_words = keep.tile([P, 2, 2 * OUT], U8, align_bytes=64)
+            w_planes = keep.tile([P, 2, OUT], U8, align_bytes=64)
+            nc.vector.memset(w_planes[:].rearrange("p w n -> p (w n)").bitcast(I32), 0)
+            for w, (words, scales) in enumerate(
+                ((lin3_W0_words, lin3_W0_scales), (lin3_W1_words, lin3_W1_scales))
+            ):
+                nc.sync.dma_start(out=w_words[:, w, :].bitcast(I32), in_=words[0].bitcast(I32))
+                for quadrant in range(4):
+                    nc.sync.dma_start(
+                        out=w_planes[32 * quadrant : 32 * quadrant + 4, w, :].bitcast(I32),
+                        in_=scales[0, 4 * quadrant : 4 * quadrant + 4, :].bitcast(I32),
+                    )
+            byp_w = keep.tile([P, 2, OUT], BF16)
+            nc.sync.dma_start(out=byp_w[:, 0, :], in_=byp_W0)
+            nc.sync.dma_start(out=byp_w[:, 1, :], in_=byp_W1)
+
+            norm_rows = keep.tile([P, P], BF16)
+            nc.vector.memset(norm_rows[:], 0.0)
+            nc.sync.dma_start(out=norm_rows[0:4, :], in_=bn_weight.rearrange("(r c) -> r c", c=P))
+            nc.sync.dma_start(out=norm_rows[4:6, :], in_=bn_bias.rearrange("(r c) -> r c", c=P))
+            norm_flipped = feat_psum.tile([P, 2, CHUNK], BF16, name="f_flipped")
+            nc.tensor.transpose(norm_flipped[:, 0, 0:P], norm_rows[:], ident_bf16[:])
+            norm_cols = keep.tile([P, 8], F32)
+            nc.vector.tensor_copy(out=norm_cols[:], in_=norm_flipped[:, 0, 0:8])
+
+            def prepare_group(c, g, operand):
+                rows = loaded[c]
+                if g == 0:
+                    words = rows["x_scalars"][:].bitcast(F32)
+
+                    def word_columns(t, u):
+                        return words[:, t, u : HID // 2 : 2]
+                else:
+                    picked = sorting.tile([P, 2, CHUNK, 2], BF16, name="picked")
+                    by_q = rows["x_vectors"][:].rearrange("p t (q r) -> p (t q) r", r=4 * DV)
+                    nc.gpsimd.tensor_scalar(
+                        out=picked[:],
+                        in0=by_q.rearrange("p m (u e d) -> p d u m e", u=2, e=2, d=DV)[:, g - 1],
+                        scalar1=1.0,
+                        scalar2=0.0,
+                        op0=MULT,
+                        op1=ADD,
+                    )
+                    words = picked[:].rearrange("p u m e -> p u (m e)").bitcast(F32)
+
+                    def word_columns(t, u):
+                        return words[:, u, t * P : (t + 1) * P]
+
+                grouped = grouping.tile([P, CHUNK, 2], F32, name="grouped", align_bytes=64)
+                for half in range(2):
+                    flipped = flip_psum.tile([P, 2, 2, P], F32, name="flipped")
+                    for u in range(2):
+                        for i in range(2):
+                            nc.tensor.transpose(
+                                flipped[:, u, i, :], word_columns(2 * half + i, u), ident_f32[:]
+                            )
+                    copy_out = nc.vector.tensor_copy if half == 0 else nc.scalar.copy
+                    copy_out(
+                        out=grouped[:, half * 2 * P : (half + 1) * 2 * P, :],
+                        in_=flipped[:].rearrange("p u i n -> p (i n) u"),
+                    )
+                nc.vector.quantize_mx(
+                    out=operand["codes"][:, g, :].bitcast(FP8X4),
+                    scales=operand["planes"][:, g, :],
+                    in_=grouped[:].rearrange("p n u -> p (n u)").bitcast(BF16),
+                )
+
+                if g % 2 == 0:
+                    operand["f_flipped"] = feat_psum.tile([P, 2, CHUNK], BF16, name="f_flipped")
+                f_flipped = operand["f_flipped"]
+                for t in range(CHUNK_TILES):
+                    if g == 0:
+                        f_columns = rows["f_rows"][:, t, 0:BYP]
+                    else:
+                        f_columns = rows["f_rows"][:, t, BYP + g - 1 : GROUPS * BYP : DV]
+                    nc.tensor.transpose(
+                        f_flipped[:, g % 2, t * P : (t + 1) * P], f_columns, ident_bf16[:]
+                    )
+                if g % 2 == 1:
+                    nc.scalar.copy(out=operand["f_cols"][:, g - 1 : g + 1, :], in_=f_flipped[:])
+
+            def new_operand():
+                return {
+                    "codes": operands.tile([P, GROUPS, CHUNK], U32, name="codes", align_bytes=64),
+                    "planes": operands.tile([P, GROUPS, CHUNK], U8, name="planes", align_bytes=64),
+                    "f_cols": operands.tile([P, GROUPS, CHUNK], BF16, name="f_cols"),
+                }
+
+            def multiply_group(c, g, operand):
+                w = min(g, 1)
+                cols = slice(c * CHUNK, (c + 1) * CHUNK)
+                for h in range(HALVES):
+                    mx_acc = mx_psum.tile([P, CHUNK], F32, name="mx_acc")
+                    nc.tensor.matmul_mx(
+                        out=mx_acc[:],
+                        lhsT=w_words[:, w, 2 * h * P : 2 * (h + 1) * P].bitcast(FP4X4),
+                        lhsT_scale=w_planes[:, w, h * P : (h + 1) * P],
+                        rhs=operand["codes"][:, g, :].bitcast(FP8X4),
+                        rhs_scale=operand["planes"][:, g, :],
+                        start=True,
+                        stop=True,
+                    )
+                    byp_acc = byp_psum.tile([P, CHUNK], F32, name="byp_acc")
+                    nc.tensor.matmul(
+                        byp_acc[:],
+                        lhsT=byp_w[:, w, h * P : (h + 1) * P],
+                        rhs=operand["f_cols"][:, g, :],
+                        start=True,
+                        stop=True,
+                    )
+                    bypass = sums.tile([P, CHUNK], F32, name="bypass")
+                    nc.scalar.mul(out=bypass[:], in_=byp_acc[:], mul=1.0 / math.sqrt(BYP))
+                    y_part = y[:, 2 * g + h, cols]
+                    nc.vector.scalar_tensor_tensor(
+                        out=y_part,
+                        in0=mx_acc[:],
+                        scalar=1.0 / math.sqrt(HID),
+                        in1=bypass[:],
+                        op0=MULT,
+                        op1=ADD,
+                    )
+                    if g == 0:
+                        nc.vector.bn_stats(out=scalar_stats[:, h, c, :], in_=y_part)
+                    else:
+                        squares = scrap.tile([P, CHUNK], F32, name="squares")
+                        nc.scalar.activation(
+                            out=squares[:],
+                            in_=y_part,
+                            func=SQUARE,
+                            accum_out=vector_squares[:, h, g - 1, c : c + 1],
+                        )
+
+            operand_of = {0: new_operand()}
+            for g in range(GROUPS):
+                prepare_group(0, g, operand_of[0])
+            for c in range(CHUNKS):
+                if c + 1 < CHUNKS:
+                    loaded[c + 1] = load_chunk(c + 1)
+                    operand_of[c + 1] = new_operand()
+                for g in range(GROUPS):
+                    if c + 1 < CHUNKS:
+                        prepare_group(c + 1, g, operand_of[c + 1])
+                    multiply_group(c, g, operand_of[c])
+
+            mean_var = keep.tile([P, HALVES, 2], F32)
+            for h in range(HALVES):
+                nc.vector.bn_aggr(
+                    out=mean_var[:, h, :], in_=scalar_stats[:, h].rearrange("p c s -> p (c s)")
+                )
+            vector_sum = keep.tile([P, HALVES], F32)
+            nc.vector.tensor_reduce(
+                out=vector_sum[:],
+                in_=vector_squares[:].rearrange("p h d c -> p h (d c)"),
+                axis=mybir.AxisListType.X,
+                op=ADD,
+            )
+            spread = keep.tile([P, 2 * HALVES], F32)
+            nc.vector.tensor_scalar(
+                out=spread[:, 0:HALVES], in0=mean_var[:, :, 1], scalar1=EPS, scalar2=None, op0=ADD
+            )
+            nc.vector.tensor_scalar(
+                out=spread[:, HALVES:],
+                in0=vector_sum[:],
+                scalar1=1.0 / (DV * NODES),
+                scalar2=EPS,
+                op0=MULT,
+                op1=ADD,
+            )
+            nc.scalar.sqrt(out=spread[:], in_=spread[:])
+            nc.vector.reciprocal(out=gain[:], in_=spread[:])
+            nc.vector.tensor_mul(out=gain[:], in0=gain[:], in1=norm_cols[:, 0 : 2 * HALVES])
+            nc.vector.tensor_mul(out=shift[:], in0=mean_var[:, :, 0], in1=gain[:, 0:HALVES])
+            nc.vector.tensor_sub(
+                out=shift[:], in0=norm_cols[:, 2 * HALVES : 3 * HALVES], in1=shift[:]
+            )
+
+        with ExitStack() as second:
+            rows_out = second.enter_context(tc.tile_pool(name="rows_out", bufs=3))
+            scalar_psum = second.enter_context(tc.psum_pool(name="scalar_psum", bufs=2))
+            vector_psum = second.enter_context(tc.psum_pool(name="vector_psum", bufs=6))
+
+            for c in range(CHUNKS):
+                cols = slice(c * CHUNK, (c + 1) * CHUNK)
+                for h in range(HALVES):
+                    nc.vector.tensor_scalar(
+                        out=y[:, h, cols],
+                        in0=y[:, h, cols],
+                        scalar1=gain[:, h : h + 1],
+                        scalar2=shift[:, h : h + 1],
+                        op0=MULT,
+                        op1=ADD,
+                    )
+                for g in range(1, GROUPS):
+                    for h in range(HALVES):
+                        nc.vector.tensor_scalar(
+                            out=y[:, 2 * g + h, cols],
+                            in0=y[:, 2 * g + h, cols],
+                            scalar1=gain[:, HALVES + h : HALVES + h + 1],
+                            scalar2=None,
+                            op0=MULT,
+                        )
+                for pair in range(CHUNK_TILES // 2):
+                    first_tile = c * CHUNK_TILES + 2 * pair
+                    result = rows_out.tile([P, 2, GROUPS * OUT], F32, name="result")
+                    scalars_t = scalar_psum.tile([P, 2, OUT], F32, name="scalars_t")
+                    for i in range(2):
+                        nodes = slice((first_tile + i) * P, (first_tile + i + 1) * P)
+                        for h in range(HALVES):
+                            nc.tensor.transpose(
+                                scalars_t[:, i, h * P : (h + 1) * P], y[:, h, nodes], ident_f32[:]
+                            )
+                    nc.vector.tensor_copy(out=result[:, :, 0:OUT], in_=scalars_t[:])
+                    for i in range(2):
+                        nodes = slice((first_tile + i) * P, (first_tile + i + 1) * P)
+                        for h in range(HALVES):
+                            vectors_t = vector_psum.tile([P, DV, P], F32, name="vectors_t")
+                            for d in range(DV):
+                                nc.tensor.transpose(
+                                    vectors_t[:, d, :], y[:, 2 * (1 + d) + h, nodes], ident_f32[:]
+                                )
+                            start = OUT + h * DV * P
+                            nc.scalar.copy(
+                                out=result[:, i, start : start + DV * P].rearrange(
+                                    "p (o d) -> p o d", d=DV
+                                ),
+                                in_=vectors_t[:].rearrange("p d o -> p o d"),
+                            )
+                    nc.sync.dma_start(
+                        out=out_tiles[:, first_tile : first_tile + 2, :], in_=result[:]
+                    )

@@ -28,6 +28,7 @@ BYP = 128
 OUT = 256
 HALVES = OUT // P
 BLOCKS = GROUPS * HALVES
+STEPS = CHUNKS * GROUPS
 EPS = 1e-5
 
 FLOPS = 2 * NODES * GROUPS * OUT * (HID + BYP)
@@ -57,7 +58,7 @@ def tile_feedforward_pb_t_kernel(
 
         y = keep.tile([P, BLOCKS, NODES], F32)
         scalar_stats = keep.tile([P, HALVES, CHUNKS, 6], F32)
-        vector_squares = keep.tile([P, HALVES, DV, CHUNKS], F32)
+        vector_squares = keep.tile([P, HALVES, CHUNKS], F32)
         gain = keep.tile([P, 2 * HALVES], F32)
         shift = keep.tile([P, HALVES], F32)
 
@@ -119,25 +120,41 @@ def tile_feedforward_pb_t_kernel(
             norm_cols = keep.tile([P, 8], F32)
             nc.vector.tensor_copy(out=norm_cols[:], in_=norm_flipped[:, 0, 0:8])
 
-            def prepare_group(c, g, operand):
+            picked_of = {}
+            grouped_of = {}
+            operand_of = {}
+
+            def sort_step(s):
+                c, g = divmod(s, GROUPS)
+                if g == 0:
+                    return
+                picked = sorting.tile([P, 2, CHUNK, 2], BF16, name="picked")
+                by_q = loaded[c]["x_vectors"][:].rearrange("p t (q r) -> p (t q) r", r=4 * DV)
+                nc.vector.tensor_copy(
+                    out=picked[:],
+                    in_=by_q.rearrange("p m (u e d) -> p d u m e", u=2, e=2, d=DV)[:, g - 1],
+                )
+                picked_of[s] = picked
+
+            def flip_step(s):
+                c, g = divmod(s, GROUPS)
+                if g == 0:
+                    if c + 1 < CHUNKS:
+                        loaded[c + 1] = load_chunk(c + 1)
+                    operand_of[c] = {
+                        "codes": operands.tile([P, GROUPS, CHUNK], U32, name="codes", align_bytes=64),
+                        "planes": operands.tile([P, GROUPS, CHUNK], U8, name="planes", align_bytes=64),
+                        "f_cols": operands.tile([P, GROUPS, CHUNK], BF16, name="f_cols"),
+                    }
                 rows = loaded[c]
+                operand = operand_of[c]
                 if g == 0:
                     words = rows["x_scalars"][:].bitcast(F32)
 
                     def word_columns(t, u):
                         return words[:, t, u : HID // 2 : 2]
                 else:
-                    picked = sorting.tile([P, 2, CHUNK, 2], BF16, name="picked")
-                    by_q = rows["x_vectors"][:].rearrange("p t (q r) -> p (t q) r", r=4 * DV)
-                    nc.gpsimd.tensor_scalar(
-                        out=picked[:],
-                        in0=by_q.rearrange("p m (u e d) -> p d u m e", u=2, e=2, d=DV)[:, g - 1],
-                        scalar1=1.0,
-                        scalar2=0.0,
-                        op0=MULT,
-                        op1=ADD,
-                    )
-                    words = picked[:].rearrange("p u m e -> p u (m e)").bitcast(F32)
+                    words = picked_of[s][:].rearrange("p u m e -> p u (m e)").bitcast(F32)
 
                     def word_columns(t, u):
                         return words[:, u, t * P : (t + 1) * P]
@@ -150,16 +167,11 @@ def tile_feedforward_pb_t_kernel(
                             nc.tensor.transpose(
                                 flipped[:, u, i, :], word_columns(2 * half + i, u), ident_f32[:]
                             )
-                    copy_out = nc.vector.tensor_copy if half == 0 else nc.scalar.copy
-                    copy_out(
+                    nc.scalar.copy(
                         out=grouped[:, half * 2 * P : (half + 1) * 2 * P, :],
                         in_=flipped[:].rearrange("p u i n -> p (i n) u"),
                     )
-                nc.vector.quantize_mx(
-                    out=operand["codes"][:, g, :].bitcast(FP8X4),
-                    scales=operand["planes"][:, g, :],
-                    in_=grouped[:].rearrange("p n u -> p (n u)").bitcast(BF16),
-                )
+                grouped_of[s] = grouped
 
                 if g % 2 == 0:
                     operand["f_flipped"] = feat_psum.tile([P, 2, CHUNK], BF16, name="f_flipped")
@@ -173,16 +185,21 @@ def tile_feedforward_pb_t_kernel(
                         f_flipped[:, g % 2, t * P : (t + 1) * P], f_columns, ident_bf16[:]
                     )
                 if g % 2 == 1:
-                    nc.scalar.copy(out=operand["f_cols"][:, g - 1 : g + 1, :], in_=f_flipped[:])
+                    nc.vector.tensor_copy(
+                        out=operand["f_cols"][:, g - 1 : g + 1, :], in_=f_flipped[:]
+                    )
 
-            def new_operand():
-                return {
-                    "codes": operands.tile([P, GROUPS, CHUNK], U32, name="codes", align_bytes=64),
-                    "planes": operands.tile([P, GROUPS, CHUNK], U8, name="planes", align_bytes=64),
-                    "f_cols": operands.tile([P, GROUPS, CHUNK], BF16, name="f_cols"),
-                }
+            def quantise_step(s):
+                c, g = divmod(s, GROUPS)
+                nc.vector.quantize_mx(
+                    out=operand_of[c]["codes"][:, g, :].bitcast(FP8X4),
+                    scales=operand_of[c]["planes"][:, g, :],
+                    in_=grouped_of[s][:].rearrange("p n u -> p (n u)").bitcast(BF16),
+                )
 
-            def multiply_group(c, g, operand):
+            def multiply_step(s):
+                c, g = divmod(s, GROUPS)
+                operand = operand_of[c]
                 w = min(g, 1)
                 cols = slice(c * CHUNK, (c + 1) * CHUNK)
                 for h in range(HALVES):
@@ -206,9 +223,8 @@ def tile_feedforward_pb_t_kernel(
                     )
                     bypass = sums.tile([P, CHUNK], F32, name="bypass")
                     nc.scalar.mul(out=bypass[:], in_=byp_acc[:], mul=1.0 / math.sqrt(BYP))
-                    y_part = y[:, 2 * g + h, cols]
                     nc.vector.scalar_tensor_tensor(
-                        out=y_part,
+                        out=y[:, 2 * g + h, cols],
                         in0=mx_acc[:],
                         scalar=1.0 / math.sqrt(HID),
                         in1=bypass[:],
@@ -216,27 +232,26 @@ def tile_feedforward_pb_t_kernel(
                         op1=ADD,
                     )
                     if g == 0:
-                        nc.vector.bn_stats(out=scalar_stats[:, h, c, :], in_=y_part)
-                    else:
-                        squares = scrap.tile([P, CHUNK], F32, name="squares")
+                        nc.vector.bn_stats(out=scalar_stats[:, h, c, :], in_=y[:, h, cols])
+                if g == GROUPS - 1:
+                    for h in range(HALVES):
+                        squares = scrap.tile([P, DV, CHUNK], BF16, name="squares")
                         nc.scalar.activation(
                             out=squares[:],
-                            in_=y_part,
+                            in_=y[:, 2 + h : BLOCKS : 2, cols],
                             func=SQUARE,
-                            accum_out=vector_squares[:, h, g - 1, c : c + 1],
+                            accum_out=vector_squares[:, h, c : c + 1],
                         )
 
-            operand_of = {0: new_operand()}
-            for g in range(GROUPS):
-                prepare_group(0, g, operand_of[0])
-            for c in range(CHUNKS):
-                if c + 1 < CHUNKS:
-                    loaded[c + 1] = load_chunk(c + 1)
-                    operand_of[c + 1] = new_operand()
-                for g in range(GROUPS):
-                    if c + 1 < CHUNKS:
-                        prepare_group(c + 1, g, operand_of[c + 1])
-                    multiply_group(c, g, operand_of[c])
+            def run(stage, s):
+                if 0 <= s < STEPS:
+                    stage(s)
+
+            for now in range(-GROUPS - 1, STEPS):
+                run(sort_step, now + GROUPS + 1)
+                run(flip_step, now + GROUPS)
+                run(quantise_step, now + GROUPS - 1)
+                run(multiply_step, now)
 
             mean_var = keep.tile([P, HALVES, 2], F32)
             for h in range(HALVES):
@@ -246,7 +261,7 @@ def tile_feedforward_pb_t_kernel(
             vector_sum = keep.tile([P, HALVES], F32)
             nc.vector.tensor_reduce(
                 out=vector_sum[:],
-                in_=vector_squares[:].rearrange("p h d c -> p h (d c)"),
+                in_=vector_squares[:],
                 axis=mybir.AxisListType.X,
                 op=ADD,
             )
@@ -286,15 +301,14 @@ def tile_feedforward_pb_t_kernel(
                         op0=MULT,
                         op1=ADD,
                     )
-                for g in range(1, GROUPS):
-                    for h in range(HALVES):
-                        nc.vector.tensor_scalar(
-                            out=y[:, 2 * g + h, cols],
-                            in0=y[:, 2 * g + h, cols],
-                            scalar1=gain[:, HALVES + h : HALVES + h + 1],
-                            scalar2=None,
-                            op0=MULT,
-                        )
+                for h in range(HALVES):
+                    nc.vector.tensor_scalar(
+                        out=y[:, 2 + h : BLOCKS : 2, cols],
+                        in0=y[:, 2 + h : BLOCKS : 2, cols],
+                        scalar1=gain[:, HALVES + h : HALVES + h + 1],
+                        scalar2=None,
+                        op0=MULT,
+                    )
                 for pair in range(CHUNK_TILES // 2):
                     first_tile = c * CHUNK_TILES + 2 * pair
                     result = rows_out.tile([P, 2, GROUPS * OUT], F32, name="result")

@@ -29,6 +29,8 @@ OUT = 256
 HALVES = OUT // P
 BLOCKS = GROUPS * HALVES
 STEPS = CHUNKS * GROUPS
+FLIP_LEAD = GROUPS
+SORT_LEAD = FLIP_LEAD + 3
 EPS = 1e-5
 
 FLOPS = 2 * NODES * GROUPS * OUT * (HID + BYP)
@@ -58,33 +60,51 @@ def tile_feedforward_pb_t_kernel(
 
         y = keep.tile([P, BLOCKS, NODES], F32)
         scalar_stats = keep.tile([P, HALVES, CHUNKS, 6], F32)
-        vector_squares = keep.tile([P, HALVES, CHUNKS], F32)
+        vector_squares = keep.tile([P, HALVES, DV, CHUNKS], F32)
         gain = keep.tile([P, 2 * HALVES], F32)
         shift = keep.tile([P, HALVES], F32)
 
         with ExitStack() as first:
             loads = first.enter_context(tc.tile_pool(name="loads", bufs=2))
-            sorting = first.enter_context(tc.tile_pool(name="sorting", bufs=3))
+            sorting = first.enter_context(tc.tile_pool(name="sorting", bufs=DV))
             grouping = first.enter_context(tc.tile_pool(name="grouping", bufs=2))
             operands = first.enter_context(tc.tile_pool(name="operands", bufs=2))
             sums = first.enter_context(tc.tile_pool(name="sums", bufs=3))
-            scrap = first.enter_context(tc.tile_pool(name="scrap", bufs=1))
-            flip_psum = first.enter_context(tc.psum_pool(name="flip_psum", bufs=3))
+            scrap = first.enter_context(tc.tile_pool(name="scrap", bufs=2))
+            flip_psum = first.enter_context(tc.psum_pool(name="flip_psum", bufs=2))
             feat_psum = first.enter_context(tc.psum_pool(name="feat_psum", bufs=1))
-            mx_psum = first.enter_context(tc.psum_pool(name="mx_psum", bufs=2))
+            mx_psum = first.enter_context(tc.psum_pool(name="mx_psum", bufs=3))
             byp_psum = first.enter_context(tc.psum_pool(name="byp_psum", bufs=2))
 
-            def load_chunk(c):
+            x_vectors_of = {}
+            x_scalars_of = {}
+            f_rows_of = {}
+            picked_of = {}
+            grouped_of = {}
+            operand_of = {}
+            product_of = {}
+
+            def load_vectors(c):
+                if c >= CHUNKS:
+                    return
+                tiles = slice(c * CHUNK_TILES, (c + 1) * CHUNK_TILES)
+                x_vectors = loads.tile([P, CHUNK_TILES, DV * HID], BF16, name="x_vectors")
+                nc.sync.dma_start(out=x_vectors[:], in_=h2_tiles[:, tiles, HID:])
+                x_vectors_of[c] = x_vectors
+
+            def load_rest(c):
+                if c >= CHUNKS:
+                    return
                 tiles = slice(c * CHUNK_TILES, (c + 1) * CHUNK_TILES)
                 x_scalars = loads.tile([P, CHUNK_TILES, HID], BF16, name="x_scalars")
                 nc.sync.dma_start(out=x_scalars[:], in_=h2_tiles[:, tiles, 0:HID])
-                x_vectors = loads.tile([P, CHUNK_TILES, DV * HID], BF16, name="x_vectors")
-                nc.sync.dma_start(out=x_vectors[:], in_=h2_tiles[:, tiles, HID:])
+                x_scalars_of[c] = x_scalars
                 f_rows = loads.tile([P, CHUNK_TILES, GROUPS * BYP], BF16, name="f_rows")
                 nc.sync.dma_start(out=f_rows[:], in_=features_tiles[:, tiles, :])
-                return {"x_scalars": x_scalars, "x_vectors": x_vectors, "f_rows": f_rows}
+                f_rows_of[c] = f_rows
 
-            loaded = {0: load_chunk(0)}
+            load_vectors(0)
+            load_rest(0)
 
             ident_f32 = keep.tile([P, P], F32)
             make_identity(nc, ident_f32[:])
@@ -120,74 +140,66 @@ def tile_feedforward_pb_t_kernel(
             norm_cols = keep.tile([P, 8], F32)
             nc.vector.tensor_copy(out=norm_cols[:], in_=norm_flipped[:, 0, 0:8])
 
-            picked_of = {}
-            grouped_of = {}
-            operand_of = {}
+            load_vectors(1)
+            load_rest(1)
+
 
             def sort_step(s):
                 c, g = divmod(s, GROUPS)
                 if g == 0:
                     return
                 picked = sorting.tile([P, 2, CHUNK, 2], BF16, name="picked")
-                by_q = loaded[c]["x_vectors"][:].rearrange("p t (q r) -> p (t q) r", r=4 * DV)
+                by_q = x_vectors_of[c][:].rearrange("p t (q r) -> p (t q) r", r=4 * DV)
                 nc.vector.tensor_copy(
                     out=picked[:],
                     in_=by_q.rearrange("p m (u e d) -> p d u m e", u=2, e=2, d=DV)[:, g - 1],
                 )
                 picked_of[s] = picked
+                if g == DV:
+                    load_vectors(c + 2)
 
-            def flip_step(s):
+            def flip_half(s, half):
                 c, g = divmod(s, GROUPS)
-                if g == 0:
-                    if c + 1 < CHUNKS:
-                        loaded[c + 1] = load_chunk(c + 1)
+                if g == 0 and half == 0:
                     operand_of[c] = {
                         "codes": operands.tile([P, GROUPS, CHUNK], U32, name="codes", align_bytes=64),
                         "planes": operands.tile([P, GROUPS, CHUNK], U8, name="planes", align_bytes=64),
                         "f_cols": operands.tile([P, GROUPS, CHUNK], BF16, name="f_cols"),
                     }
-                rows = loaded[c]
                 operand = operand_of[c]
-                if g == 0:
-                    words = rows["x_scalars"][:].bitcast(F32)
-
-                    def word_columns(t, u):
-                        return words[:, t, u : HID // 2 : 2]
-                else:
-                    words = picked_of[s][:].rearrange("p u m e -> p u (m e)").bitcast(F32)
-
-                    def word_columns(t, u):
-                        return words[:, u, t * P : (t + 1) * P]
-
-                grouped = grouping.tile([P, CHUNK, 2], F32, name="grouped", align_bytes=64)
-                for half in range(2):
-                    flipped = flip_psum.tile([P, 2, 2, P], F32, name="flipped")
-                    for u in range(2):
-                        for i in range(2):
-                            nc.tensor.transpose(
-                                flipped[:, u, i, :], word_columns(2 * half + i, u), ident_f32[:]
-                            )
-                    nc.scalar.copy(
-                        out=grouped[:, half * 2 * P : (half + 1) * 2 * P, :],
-                        in_=flipped[:].rearrange("p u i n -> p (i n) u"),
-                    )
-                grouped_of[s] = grouped
-
-                if g % 2 == 0:
+                node_tiles = range(2 * half, 2 * half + 2)
+                flipped = flip_psum.tile([P, 2, 2, P], F32, name="flipped")
+                for u in range(2):
+                    for t in node_tiles:
+                        if g == 0:
+                            words = x_scalars_of[c][:, t, :].bitcast(F32)[:, u : HID // 2 : 2]
+                        else:
+                            words = picked_of[s][:, u, t * P : (t + 1) * P, :]
+                            words = words.rearrange("p q e -> p (q e)").bitcast(F32)
+                        nc.tensor.transpose(flipped[:, u, t - 2 * half, :], words, ident_f32[:])
+                if half == 0:
+                    grouped_of[s] = grouping.tile([P, CHUNK, 2], F32, name="grouped", align_bytes=64)
+                nc.scalar.copy(
+                    out=grouped_of[s][:, half * 2 * P : (half + 1) * 2 * P, :],
+                    in_=flipped[:].rearrange("p u i n -> p (i n) u"),
+                )
+                if g % 2 == 0 and half == 0:
                     operand["f_flipped"] = feat_psum.tile([P, 2, CHUNK], BF16, name="f_flipped")
                 f_flipped = operand["f_flipped"]
-                for t in range(CHUNK_TILES):
+                for t in node_tiles:
                     if g == 0:
-                        f_columns = rows["f_rows"][:, t, 0:BYP]
+                        f_columns = f_rows_of[c][:, t, 0:BYP]
                     else:
-                        f_columns = rows["f_rows"][:, t, BYP + g - 1 : GROUPS * BYP : DV]
+                        f_columns = f_rows_of[c][:, t, BYP + g - 1 : GROUPS * BYP : DV]
                     nc.tensor.transpose(
                         f_flipped[:, g % 2, t * P : (t + 1) * P], f_columns, ident_bf16[:]
                     )
-                if g % 2 == 1:
+                if g % 2 == 1 and half == 1:
                     nc.vector.tensor_copy(
                         out=operand["f_cols"][:, g - 1 : g + 1, :], in_=f_flipped[:]
                     )
+                if g == DV and half == 1:
+                    load_rest(c + 2)
 
             def quantise_step(s):
                 c, g = divmod(s, GROUPS)
@@ -197,61 +209,75 @@ def tile_feedforward_pb_t_kernel(
                     in_=grouped_of[s][:].rearrange("p n u -> p (n u)").bitcast(BF16),
                 )
 
-            def multiply_step(s):
+            def multiply_half(s, h):
                 c, g = divmod(s, GROUPS)
                 operand = operand_of[c]
                 w = min(g, 1)
-                cols = slice(c * CHUNK, (c + 1) * CHUNK)
+                mx_acc = mx_psum.tile([P, CHUNK], F32, name="mx_acc")
+                nc.tensor.matmul_mx(
+                    out=mx_acc[:],
+                    lhsT=w_words[:, w, 2 * h * P : 2 * (h + 1) * P].bitcast(FP4X4),
+                    lhsT_scale=w_planes[:, w, h * P : (h + 1) * P],
+                    rhs=operand["codes"][:, g, :].bitcast(FP8X4),
+                    rhs_scale=operand["planes"][:, g, :],
+                    start=True,
+                    stop=True,
+                )
+                byp_acc = byp_psum.tile([P, CHUNK], F32, name="byp_acc")
+                nc.tensor.matmul(
+                    byp_acc[:],
+                    lhsT=byp_w[:, w, h * P : (h + 1) * P],
+                    rhs=operand["f_cols"][:, g, :],
+                    start=True,
+                    stop=True,
+                )
+                bypass = sums.tile([P, CHUNK], F32, name="bypass")
+                nc.scalar.mul(out=bypass[:], in_=byp_acc[:], mul=1.0 / math.sqrt(BYP))
+                product_of[(s, h)] = (mx_acc, bypass)
+
+            def add_half(s, h):
+                c, g = divmod(s, GROUPS)
+                mx_acc, bypass = product_of[(s, h)]
+                y_part = y[:, 2 * g + h, c * CHUNK : (c + 1) * CHUNK]
+                nc.vector.scalar_tensor_tensor(
+                    out=y_part,
+                    in0=mx_acc[:],
+                    scalar=1.0 / math.sqrt(HID),
+                    in1=bypass[:],
+                    op0=MULT,
+                    op1=ADD,
+                )
+                if g == 0:
+                    nc.vector.bn_stats(out=scalar_stats[:, h, c, :], in_=y_part)
+
+            def square_step(s):
+                c, g = divmod(s, GROUPS)
+                if g == 0:
+                    return
                 for h in range(HALVES):
-                    mx_acc = mx_psum.tile([P, CHUNK], F32, name="mx_acc")
-                    nc.tensor.matmul_mx(
-                        out=mx_acc[:],
-                        lhsT=w_words[:, w, 2 * h * P : 2 * (h + 1) * P].bitcast(FP4X4),
-                        lhsT_scale=w_planes[:, w, h * P : (h + 1) * P],
-                        rhs=operand["codes"][:, g, :].bitcast(FP8X4),
-                        rhs_scale=operand["planes"][:, g, :],
-                        start=True,
-                        stop=True,
+                    squares = scrap.tile([P, CHUNK], BF16, name="squares")
+                    nc.scalar.activation(
+                        out=squares[:],
+                        in_=y[:, 2 * g + h, c * CHUNK : (c + 1) * CHUNK],
+                        func=SQUARE,
+                        accum_out=vector_squares[:, h, g - 1, c : c + 1],
                     )
-                    byp_acc = byp_psum.tile([P, CHUNK], F32, name="byp_acc")
-                    nc.tensor.matmul(
-                        byp_acc[:],
-                        lhsT=byp_w[:, w, h * P : (h + 1) * P],
-                        rhs=operand["f_cols"][:, g, :],
-                        start=True,
-                        stop=True,
-                    )
-                    bypass = sums.tile([P, CHUNK], F32, name="bypass")
-                    nc.scalar.mul(out=bypass[:], in_=byp_acc[:], mul=1.0 / math.sqrt(BYP))
-                    nc.vector.scalar_tensor_tensor(
-                        out=y[:, 2 * g + h, cols],
-                        in0=mx_acc[:],
-                        scalar=1.0 / math.sqrt(HID),
-                        in1=bypass[:],
-                        op0=MULT,
-                        op1=ADD,
-                    )
-                    if g == 0:
-                        nc.vector.bn_stats(out=scalar_stats[:, h, c, :], in_=y[:, h, cols])
-                if g == GROUPS - 1:
-                    for h in range(HALVES):
-                        squares = scrap.tile([P, DV, CHUNK], BF16, name="squares")
-                        nc.scalar.activation(
-                            out=squares[:],
-                            in_=y[:, 2 + h : BLOCKS : 2, cols],
-                            func=SQUARE,
-                            accum_out=vector_squares[:, h, c : c + 1],
-                        )
 
-            def run(stage, s):
+            def run(stage, s, *part):
                 if 0 <= s < STEPS:
-                    stage(s)
+                    stage(s, *part)
 
-            for now in range(-GROUPS - 1, STEPS):
-                run(sort_step, now + GROUPS + 1)
-                run(flip_step, now + GROUPS)
-                run(quantise_step, now + GROUPS - 1)
-                run(multiply_step, now)
+            with tc.manual_schedule():
+                for now in range(-SORT_LEAD, STEPS + 1):
+                    run(sort_step, now + SORT_LEAD)
+                    run(flip_half, now + FLIP_LEAD, 0)
+                    run(multiply_half, now, 0)
+                    run(flip_half, now + FLIP_LEAD, 1)
+                    run(quantise_step, now + FLIP_LEAD - 1)
+                    run(add_half, now, 0)
+                    run(multiply_half, now, 1)
+                    run(add_half, now, 1)
+                    run(square_step, now - 1)
 
             mean_var = keep.tile([P, HALVES, 2], F32)
             for h in range(HALVES):
@@ -261,7 +287,7 @@ def tile_feedforward_pb_t_kernel(
             vector_sum = keep.tile([P, HALVES], F32)
             nc.vector.tensor_reduce(
                 out=vector_sum[:],
-                in_=vector_squares[:],
+                in_=vector_squares[:].rearrange("p h d c -> p h (d c)"),
                 axis=mybir.AxisListType.X,
                 op=ADD,
             )
@@ -290,7 +316,7 @@ def tile_feedforward_pb_t_kernel(
             scalar_psum = second.enter_context(tc.psum_pool(name="scalar_psum", bufs=2))
             vector_psum = second.enter_context(tc.psum_pool(name="vector_psum", bufs=6))
 
-            for c in range(CHUNKS):
+            def normalise_chunk(c):
                 cols = slice(c * CHUNK, (c + 1) * CHUNK)
                 for h in range(HALVES):
                     nc.vector.tensor_scalar(
@@ -309,32 +335,38 @@ def tile_feedforward_pb_t_kernel(
                         scalar2=None,
                         op0=MULT,
                     )
-                for pair in range(CHUNK_TILES // 2):
-                    first_tile = c * CHUNK_TILES + 2 * pair
-                    result = rows_out.tile([P, 2, GROUPS * OUT], F32, name="result")
-                    scalars_t = scalar_psum.tile([P, 2, OUT], F32, name="scalars_t")
-                    for i in range(2):
-                        nodes = slice((first_tile + i) * P, (first_tile + i + 1) * P)
-                        for h in range(HALVES):
+
+            def store_pair(first_tile):
+                result = rows_out.tile([P, 2, GROUPS * OUT], F32, name="result")
+                scalars_t = scalar_psum.tile([P, 2, OUT], F32, name="scalars_t")
+                for i in range(2):
+                    nodes = slice((first_tile + i) * P, (first_tile + i + 1) * P)
+                    for h in range(HALVES):
+                        nc.tensor.transpose(
+                            scalars_t[:, i, h * P : (h + 1) * P], y[:, h, nodes], ident_f32[:]
+                        )
+                nc.vector.tensor_copy(out=result[:, :, 0:OUT], in_=scalars_t[:])
+                for i in range(2):
+                    nodes = slice((first_tile + i) * P, (first_tile + i + 1) * P)
+                    for h in range(HALVES):
+                        vectors_t = vector_psum.tile([P, DV, P], F32, name="vectors_t")
+                        for d in range(DV):
                             nc.tensor.transpose(
-                                scalars_t[:, i, h * P : (h + 1) * P], y[:, h, nodes], ident_f32[:]
+                                vectors_t[:, d, :], y[:, 2 * (1 + d) + h, nodes], ident_f32[:]
                             )
-                    nc.vector.tensor_copy(out=result[:, :, 0:OUT], in_=scalars_t[:])
-                    for i in range(2):
-                        nodes = slice((first_tile + i) * P, (first_tile + i + 1) * P)
-                        for h in range(HALVES):
-                            vectors_t = vector_psum.tile([P, DV, P], F32, name="vectors_t")
-                            for d in range(DV):
-                                nc.tensor.transpose(
-                                    vectors_t[:, d, :], y[:, 2 * (1 + d) + h, nodes], ident_f32[:]
-                                )
-                            start = OUT + h * DV * P
-                            nc.scalar.copy(
-                                out=result[:, i, start : start + DV * P].rearrange(
-                                    "p (o d) -> p o d", d=DV
-                                ),
-                                in_=vectors_t[:].rearrange("p d o -> p o d"),
-                            )
-                    nc.sync.dma_start(
-                        out=out_tiles[:, first_tile : first_tile + 2, :], in_=result[:]
-                    )
+                        start = OUT + h * DV * P
+                        nc.scalar.copy(
+                            out=result[:, i, start : start + DV * P].rearrange(
+                                "p (o d) -> p o d", d=DV
+                            ),
+                            in_=vectors_t[:].rearrange("p d o -> p o d"),
+                        )
+                nc.sync.dma_start(out=out_tiles[:, first_tile : first_tile + 2, :], in_=result[:])
+
+            with tc.manual_schedule():
+                normalise_chunk(0)
+                for c in range(CHUNKS):
+                    store_pair(c * CHUNK_TILES)
+                    if c + 1 < CHUNKS:
+                        normalise_chunk(c + 1)
+                    store_pair(c * CHUNK_TILES + 2)

@@ -28,9 +28,14 @@ BYP = 128
 OUT = 256
 HALVES = OUT // P
 BLOCKS = GROUPS * HALVES
-STEPS = CHUNKS * GROUPS
-FLIP_LEAD = GROUPS
-SORT_LEAD = FLIP_LEAD + 3
+VECTOR_STEPS = CHUNKS * DV
+STEPS = VECTOR_STEPS + CHUNKS
+FLIP_LEAD = 4
+SORT_LEAD = FLIP_LEAD + 2
+LAST_VECTOR_INPUT = VECTOR_STEPS - FLIP_LEAD
+LATE = 1
+EARLY = 1 - LATE
+PAIRS = NODE_TILES // 2
 EPS = 1e-5
 
 FLOPS = 2 * NODES * GROUPS * OUT * (HID + BYP)
@@ -57,32 +62,50 @@ def tile_feedforward_pb_t_kernel(
 
     with ExitStack() as whole:
         keep = whole.enter_context(tc.tile_pool(name="keep", bufs=1))
+        scalar_in = whole.enter_context(tc.tile_pool(name="scalar_in", bufs=2))
+        grouping = whole.enter_context(tc.tile_pool(name="grouping", bufs=2))
+        quantised = whole.enter_context(tc.tile_pool(name="quantised", bufs=FLIP_LEAD + 1))
+        bypass_in = whole.enter_context(tc.tile_pool(name="bypass_in", bufs=2))
+        sums = whole.enter_context(tc.tile_pool(name="sums", bufs=3))
+        scrap = whole.enter_context(tc.tile_pool(name="scrap", bufs=2))
+        banks = whole.enter_context(tc.psum_pool(name="banks", bufs=1))
+
+        def bank(index, shape, dtype):
+            return banks.tile(shape, dtype, name="bank%d" % index)
 
         y = keep.tile([P, BLOCKS, NODES], F32)
         scalar_stats = keep.tile([P, HALVES, CHUNKS, 6], F32)
         vector_squares = keep.tile([P, HALVES, DV, CHUNKS], F32)
         gain = keep.tile([P, 2 * HALVES], F32)
         shift = keep.tile([P, HALVES], F32)
+        f_cols_scalar = keep.tile([P, CHUNKS, CHUNK], BF16)
 
-        with ExitStack() as first:
-            loads = first.enter_context(tc.tile_pool(name="loads", bufs=2))
-            sorting = first.enter_context(tc.tile_pool(name="sorting", bufs=DV))
-            grouping = first.enter_context(tc.tile_pool(name="grouping", bufs=2))
-            operands = first.enter_context(tc.tile_pool(name="operands", bufs=2))
-            sums = first.enter_context(tc.tile_pool(name="sums", bufs=3))
-            scrap = first.enter_context(tc.tile_pool(name="scrap", bufs=2))
-            flip_psum = first.enter_context(tc.psum_pool(name="flip_psum", bufs=2))
-            feat_psum = first.enter_context(tc.psum_pool(name="feat_psum", bufs=1))
-            mx_psum = first.enter_context(tc.psum_pool(name="mx_psum", bufs=3))
-            byp_psum = first.enter_context(tc.psum_pool(name="byp_psum", bufs=2))
+        x_vectors_of = {}
+        x_scalars_of = {}
+        f_rows_of = {}
+        picked_of = {}
+        grouped_of = {}
+        f_flipped_of = {}
+        f_cols_of = {}
+        operand_of = {}
+        product_of = {}
 
-            x_vectors_of = {}
-            x_scalars_of = {}
-            f_rows_of = {}
-            picked_of = {}
-            grouped_of = {}
-            operand_of = {}
-            product_of = {}
+        def place(s):
+            if s < VECTOR_STEPS:
+                return s // DV, 1 + s % DV
+            return s - VECTOR_STEPS, 0
+
+        def load_scalars(c):
+            if c >= CHUNKS:
+                return
+            tiles = slice(c * CHUNK_TILES, (c + 1) * CHUNK_TILES)
+            x_scalars = scalar_in.tile([P, CHUNK_TILES, HID], BF16, name="x_scalars")
+            nc.sync.dma_start(out=x_scalars[:], in_=h2_tiles[:, tiles, 0:HID])
+            x_scalars_of[c] = x_scalars
+
+        with ExitStack() as vector_input:
+            loads = vector_input.enter_context(tc.tile_pool(name="loads", bufs=2))
+            sorting = vector_input.enter_context(tc.tile_pool(name="sorting", bufs=DV))
 
             def load_vectors(c):
                 if c >= CHUNKS:
@@ -92,19 +115,16 @@ def tile_feedforward_pb_t_kernel(
                 nc.sync.dma_start(out=x_vectors[:], in_=h2_tiles[:, tiles, HID:])
                 x_vectors_of[c] = x_vectors
 
-            def load_rest(c):
+            def load_features(c):
                 if c >= CHUNKS:
                     return
                 tiles = slice(c * CHUNK_TILES, (c + 1) * CHUNK_TILES)
-                x_scalars = loads.tile([P, CHUNK_TILES, HID], BF16, name="x_scalars")
-                nc.sync.dma_start(out=x_scalars[:], in_=h2_tiles[:, tiles, 0:HID])
-                x_scalars_of[c] = x_scalars
                 f_rows = loads.tile([P, CHUNK_TILES, GROUPS * BYP], BF16, name="f_rows")
                 nc.sync.dma_start(out=f_rows[:], in_=features_tiles[:, tiles, :])
                 f_rows_of[c] = f_rows
 
             load_vectors(0)
-            load_rest(0)
+            load_features(0)
 
             ident_f32 = keep.tile([P, P], F32)
             make_identity(nc, ident_f32[:])
@@ -135,17 +155,18 @@ def tile_feedforward_pb_t_kernel(
             nc.vector.memset(norm_rows[:], 0.0)
             nc.sync.dma_start(out=norm_rows[0:4, :], in_=bn_weight.rearrange("(r c) -> r c", c=P))
             nc.sync.dma_start(out=norm_rows[4:6, :], in_=bn_bias.rearrange("(r c) -> r c", c=P))
-            norm_flipped = feat_psum.tile([P, 2, CHUNK], BF16, name="f_flipped")
-            nc.tensor.transpose(norm_flipped[:, 0, 0:P], norm_rows[:], ident_bf16[:])
+            norm_flipped = bank(2, [P, P], BF16)
+            nc.tensor.transpose(norm_flipped[:], norm_rows[:], ident_bf16[:])
             norm_cols = keep.tile([P, 8], F32)
-            nc.vector.tensor_copy(out=norm_cols[:], in_=norm_flipped[:, 0, 0:8])
+            nc.vector.tensor_copy(out=norm_cols[:], in_=norm_flipped[:, 0:8])
 
             load_vectors(1)
-            load_rest(1)
-
+            load_features(1)
+            load_scalars(0)
+            load_scalars(1)
 
             def sort_step(s):
-                c, g = divmod(s, GROUPS)
+                c, g = place(s)
                 if g == 0:
                     return
                 picked = sorting.tile([P, 2, CHUNK, 2], BF16, name="picked")
@@ -158,19 +179,36 @@ def tile_feedforward_pb_t_kernel(
                 if g == DV:
                     load_vectors(c + 2)
 
+            def flip_features(s, half):
+                c, g = place(s)
+                fill = 0 if g == 1 else 1
+                if half == 0 and g != DV:
+                    f_flipped_of[(c, fill)] = bank(2, [P, 2, CHUNK], BF16)
+                f_flipped = f_flipped_of[(c, fill)]
+                for group in ((0, 1) if g == 1 else (g,)):
+                    for t in range(2 * half, 2 * half + 2):
+                        if group == 0:
+                            f_columns = f_rows_of[c][:, t, 0:BYP]
+                        else:
+                            f_columns = f_rows_of[c][:, t, BYP + group - 1 : GROUPS * BYP : DV]
+                        nc.tensor.transpose(
+                            f_flipped[:, group % 2, t * P : (t + 1) * P], f_columns, ident_bf16[:]
+                        )
+                if half == 0:
+                    return
+                if g == 1:
+                    f_cols_of[c] = bypass_in.tile([P, DV, CHUNK], BF16, name="f_cols")
+                    nc.vector.tensor_copy(out=f_cols_scalar[:, c, :], in_=f_flipped[:, 0, :])
+                    nc.vector.tensor_copy(out=f_cols_of[c][:, 0, :], in_=f_flipped[:, 1, :])
+                if g == DV:
+                    nc.vector.tensor_copy(out=f_cols_of[c][:, 1:DV, :], in_=f_flipped[:])
+                    load_features(c + 2)
+
             def flip_half(s, half):
-                c, g = divmod(s, GROUPS)
-                if g == 0 and half == 0:
-                    operand_of[c] = {
-                        "codes": operands.tile([P, GROUPS, CHUNK], U32, name="codes", align_bytes=64),
-                        "planes": operands.tile([P, GROUPS, CHUNK], U8, name="planes", align_bytes=64),
-                        "f_cols": operands.tile([P, GROUPS, CHUNK], BF16, name="f_cols"),
-                    }
-                operand = operand_of[c]
-                node_tiles = range(2 * half, 2 * half + 2)
-                flipped = flip_psum.tile([P, 2, 2, P], F32, name="flipped")
+                c, g = place(s)
+                flipped = bank(half, [P, 2, 2, P], F32)
                 for u in range(2):
-                    for t in node_tiles:
+                    for t in range(2 * half, 2 * half + 2):
                         if g == 0:
                             words = x_scalars_of[c][:, t, :].bitcast(F32)[:, u : HID // 2 : 2]
                         else:
@@ -183,51 +221,40 @@ def tile_feedforward_pb_t_kernel(
                     out=grouped_of[s][:, half * 2 * P : (half + 1) * 2 * P, :],
                     in_=flipped[:].rearrange("p u i n -> p (i n) u"),
                 )
-                if g % 2 == 0 and half == 0:
-                    operand["f_flipped"] = feat_psum.tile([P, 2, CHUNK], BF16, name="f_flipped")
-                f_flipped = operand["f_flipped"]
-                for t in node_tiles:
-                    if g == 0:
-                        f_columns = f_rows_of[c][:, t, 0:BYP]
-                    else:
-                        f_columns = f_rows_of[c][:, t, BYP + g - 1 : GROUPS * BYP : DV]
-                    nc.tensor.transpose(
-                        f_flipped[:, g % 2, t * P : (t + 1) * P], f_columns, ident_bf16[:]
-                    )
-                if g % 2 == 1 and half == 1:
-                    nc.vector.tensor_copy(
-                        out=operand["f_cols"][:, g - 1 : g + 1, :], in_=f_flipped[:]
-                    )
-                if g == DV and half == 1:
-                    load_rest(c + 2)
+                if g > 0:
+                    flip_features(s, half)
+                elif half == 1:
+                    load_scalars(c + 2)
 
             def quantise_step(s):
-                c, g = divmod(s, GROUPS)
+                codes = quantised.tile([P, CHUNK], U32, name="codes", align_bytes=64)
+                planes = quantised.tile([P, CHUNK], U8, name="planes", align_bytes=64)
                 nc.vector.quantize_mx(
-                    out=operand_of[c]["codes"][:, g, :].bitcast(FP8X4),
-                    scales=operand_of[c]["planes"][:, g, :],
+                    out=codes[:].bitcast(FP8X4),
+                    scales=planes[:],
                     in_=grouped_of[s][:].rearrange("p n u -> p (n u)").bitcast(BF16),
                 )
+                operand_of[s] = (codes, planes)
 
             def multiply_half(s, h):
-                c, g = divmod(s, GROUPS)
-                operand = operand_of[c]
+                c, g = place(s)
+                codes, planes = operand_of[s]
                 w = min(g, 1)
-                mx_acc = mx_psum.tile([P, CHUNK], F32, name="mx_acc")
+                mx_acc = bank(3 + (2 * s + h) % 3 if g > 0 else 3 + h, [P, CHUNK], F32)
                 nc.tensor.matmul_mx(
                     out=mx_acc[:],
                     lhsT=w_words[:, w, 2 * h * P : 2 * (h + 1) * P].bitcast(FP4X4),
                     lhsT_scale=w_planes[:, w, h * P : (h + 1) * P],
-                    rhs=operand["codes"][:, g, :].bitcast(FP8X4),
-                    rhs_scale=operand["planes"][:, g, :],
+                    rhs=codes[:].bitcast(FP8X4),
+                    rhs_scale=planes[:],
                     start=True,
                     stop=True,
                 )
-                byp_acc = byp_psum.tile([P, CHUNK], F32, name="byp_acc")
+                byp_acc = bank(6 + h if g > 0 else 6, [P, CHUNK], F32)
                 nc.tensor.matmul(
                     byp_acc[:],
                     lhsT=byp_w[:, w, h * P : (h + 1) * P],
-                    rhs=operand["f_cols"][:, g, :],
+                    rhs=f_cols_of[c][:, g - 1, :] if g > 0 else f_cols_scalar[:, c, :],
                     start=True,
                     stop=True,
                 )
@@ -236,87 +263,176 @@ def tile_feedforward_pb_t_kernel(
                 product_of[(s, h)] = (mx_acc, bypass)
 
             def add_half(s, h):
-                c, g = divmod(s, GROUPS)
+                c, g = place(s)
                 mx_acc, bypass = product_of[(s, h)]
-                y_part = y[:, 2 * g + h, c * CHUNK : (c + 1) * CHUNK]
                 nc.vector.scalar_tensor_tensor(
-                    out=y_part,
+                    out=y[:, 2 * g + h, c * CHUNK : (c + 1) * CHUNK],
                     in0=mx_acc[:],
                     scalar=1.0 / math.sqrt(HID),
                     in1=bypass[:],
                     op0=MULT,
                     op1=ADD,
                 )
-                if g == 0:
-                    nc.vector.bn_stats(out=scalar_stats[:, h, c, :], in_=y_part)
 
-            def square_step(s):
-                c, g = divmod(s, GROUPS)
-                if g == 0:
-                    return
+            def measure_step(s):
+                c, g = place(s)
                 for h in range(HALVES):
-                    squares = scrap.tile([P, CHUNK], BF16, name="squares")
-                    nc.scalar.activation(
-                        out=squares[:],
-                        in_=y[:, 2 * g + h, c * CHUNK : (c + 1) * CHUNK],
-                        func=SQUARE,
-                        accum_out=vector_squares[:, h, g - 1, c : c + 1],
-                    )
+                    y_part = y[:, 2 * g + h, c * CHUNK : (c + 1) * CHUNK]
+                    if g == 0:
+                        nc.vector.bn_stats(out=scalar_stats[:, h, c, :], in_=y_part)
+                    else:
+                        squares = scrap.tile([P, CHUNK], BF16, name="squares")
+                        nc.scalar.activation(
+                            out=squares[:],
+                            in_=y_part,
+                            func=SQUARE,
+                            accum_out=vector_squares[:, h, g - 1, c : c + 1],
+                        )
 
             def run(stage, s, *part):
                 if 0 <= s < STEPS:
                     stage(s, *part)
 
+            def nothing():
+                return
+
+            def iteration(now, between=(nothing, nothing, nothing, nothing)):
+                run(sort_step, now + SORT_LEAD)
+                run(flip_half, now + FLIP_LEAD, 0)
+                run(multiply_half, now, 0)
+                between[0]()
+                run(flip_half, now + FLIP_LEAD, 1)
+                run(quantise_step, now + FLIP_LEAD - 1)
+                run(add_half, now, 0)
+                between[1]()
+                run(multiply_half, now, 1)
+                between[2]()
+                run(add_half, now, 1)
+                if now - 1 < VECTOR_STEPS:
+                    run(measure_step, now - 1)
+                if now >= VECTOR_STEPS:
+                    run(measure_step, now)
+                between[3]()
+
             with tc.manual_schedule():
-                for now in range(-SORT_LEAD, STEPS + 1):
-                    run(sort_step, now + SORT_LEAD)
-                    run(flip_half, now + FLIP_LEAD, 0)
-                    run(multiply_half, now, 0)
-                    run(flip_half, now + FLIP_LEAD, 1)
-                    run(quantise_step, now + FLIP_LEAD - 1)
-                    run(add_half, now, 0)
-                    run(multiply_half, now, 1)
-                    run(add_half, now, 1)
-                    run(square_step, now - 1)
+                for now in range(-SORT_LEAD, LAST_VECTOR_INPUT):
+                    iteration(now)
 
-            mean_var = keep.tile([P, HALVES, 2], F32)
-            for h in range(HALVES):
-                nc.vector.bn_aggr(
-                    out=mean_var[:, h, :], in_=scalar_stats[:, h].rearrange("p c s -> p (c s)")
-                )
+        with ExitStack() as storing:
+            rows_out = storing.enter_context(tc.tile_pool(name="rows_out", bufs=3))
+            turn = {"bank": 0}
+
+            def next_bank(free_banks, shape):
+                turn["bank"] = turn["bank"] + 1
+                return bank(free_banks[turn["bank"] % len(free_banks)], shape, F32)
+
             vector_sum = keep.tile([P, HALVES], F32)
-            nc.vector.tensor_reduce(
-                out=vector_sum[:],
-                in_=vector_squares[:].rearrange("p h d c -> p h (d c)"),
-                axis=mybir.AxisListType.X,
-                op=ADD,
-            )
             spread = keep.tile([P, 2 * HALVES], F32)
-            nc.vector.tensor_scalar(
-                out=spread[:, 0:HALVES], in0=mean_var[:, :, 1], scalar1=EPS, scalar2=None, op0=ADD
-            )
-            nc.vector.tensor_scalar(
-                out=spread[:, HALVES:],
-                in0=vector_sum[:],
-                scalar1=1.0 / (DV * NODES),
-                scalar2=EPS,
-                op0=MULT,
-                op1=ADD,
-            )
-            nc.scalar.sqrt(out=spread[:], in_=spread[:])
-            nc.vector.reciprocal(out=gain[:], in_=spread[:])
-            nc.vector.tensor_mul(out=gain[:], in0=gain[:], in1=norm_cols[:, 0 : 2 * HALVES])
-            nc.vector.tensor_mul(out=shift[:], in0=mean_var[:, :, 0], in1=gain[:, 0:HALVES])
-            nc.vector.tensor_sub(
-                out=shift[:], in0=norm_cols[:, 2 * HALVES : 3 * HALVES], in1=shift[:]
-            )
+            gain_square = keep.tile([P, P], F32)
+            gain_rows = keep.tile([P, P, DV], F32)
+            mean_var = keep.tile([P, HALVES, 2], F32)
 
-        with ExitStack() as second:
-            rows_out = second.enter_context(tc.tile_pool(name="rows_out", bufs=3))
-            scalar_psum = second.enter_context(tc.psum_pool(name="scalar_psum", bufs=2))
-            vector_psum = second.enter_context(tc.psum_pool(name="vector_psum", bufs=6))
+            def vector_spread():
+                nc.vector.tensor_reduce(
+                    out=vector_sum[:],
+                    in_=vector_squares[:].rearrange("p h d c -> p h (d c)"),
+                    axis=mybir.AxisListType.X,
+                    op=ADD,
+                )
+                nc.vector.tensor_scalar(
+                    out=spread[:, HALVES:],
+                    in0=vector_sum[:],
+                    scalar1=1.0 / (DV * NODES),
+                    scalar2=EPS,
+                    op0=MULT,
+                    op1=ADD,
+                )
 
-            def normalise_chunk(c):
+            def vector_root():
+                nc.scalar.sqrt(out=spread[:, HALVES:], in_=spread[:, HALVES:])
+
+            def vector_gain():
+                nc.vector.reciprocal(out=gain[:, HALVES:], in_=spread[:, HALVES:])
+                nc.vector.tensor_mul(
+                    out=gain[:, HALVES:], in0=gain[:, HALVES:], in1=norm_cols[:, HALVES : 2 * HALVES]
+                )
+                nc.vector.tensor_copy(
+                    out=gain_square[:],
+                    in_=gain[:, HALVES + LATE : HALVES + LATE + 1].to_broadcast([P, P]),
+                )
+                normalise_pair(0)
+                normalise_pair(1)
+
+            def flip_gain():
+                gain_flipped = bank(5, [P, P], F32)
+                nc.tensor.transpose(gain_flipped[:], gain_square[:], ident_f32[:])
+                product_of["gain"] = gain_flipped
+
+            def spread_gain():
+                nc.vector.tensor_copy(
+                    out=gain_rows[:],
+                    in_=product_of["gain"][:].unsqueeze(2).to_broadcast([P, P, DV]),
+                )
+
+            def normalise_pair(pair):
+                if pair >= PAIRS:
+                    return
+                cols = slice(2 * pair * P, 2 * (pair + 1) * P)
+                nc.gpsimd.tensor_scalar(
+                    out=y[:, 2 + EARLY : BLOCKS : 2, cols],
+                    in0=y[:, 2 + EARLY : BLOCKS : 2, cols],
+                    scalar1=gain[:, HALVES + EARLY : HALVES + EARLY + 1],
+                    scalar2=0.0,
+                    op0=MULT,
+                    op1=ADD,
+                )
+
+            def store_vectors(pair, free_banks):
+                normalise_pair(pair + 2)
+                rows = rows_out.tile([P, 2, DV * OUT], F32, name="vector_rows")
+                for i in range(2):
+                    nodes = slice((2 * pair + i) * P, (2 * pair + i + 1) * P)
+                    for h in (LATE, EARLY):
+                        vectors_t = next_bank(free_banks, [P, DV, P])
+                        for d in range(DV):
+                            nc.tensor.transpose(
+                                vectors_t[:, d, :], y[:, 2 * (1 + d) + h, nodes], ident_f32[:]
+                            )
+                        part = rows[:, i, h * DV * P : (h + 1) * DV * P].rearrange(
+                            "p (o d) -> p o d", d=DV
+                        )
+                        if h == LATE:
+                            nc.vector.tensor_tensor(
+                                out=part,
+                                in0=vectors_t[:].rearrange("p d o -> p o d"),
+                                in1=gain_rows[:],
+                                op=MULT,
+                            )
+                        else:
+                            nc.scalar.copy(out=part, in_=vectors_t[:].rearrange("p d o -> p o d"))
+                nc.sync.dma_start(out=out_tiles[:, 2 * pair : 2 * pair + 2, OUT:], in_=rows[:])
+
+            def scalar_gain():
+                for h in range(HALVES):
+                    nc.vector.bn_aggr(
+                        out=mean_var[:, h, :], in_=scalar_stats[:, h].rearrange("p c s -> p (c s)")
+                    )
+                nc.vector.tensor_scalar(
+                    out=spread[:, 0:HALVES], in0=mean_var[:, :, 1], scalar1=EPS, scalar2=None, op0=ADD
+                )
+                nc.scalar.sqrt(out=spread[:, 0:HALVES], in_=spread[:, 0:HALVES])
+                nc.vector.reciprocal(out=gain[:, 0:HALVES], in_=spread[:, 0:HALVES])
+                nc.vector.tensor_mul(
+                    out=gain[:, 0:HALVES], in0=gain[:, 0:HALVES], in1=norm_cols[:, 0:HALVES]
+                )
+                nc.vector.tensor_mul(out=shift[:], in0=mean_var[:, :, 0], in1=gain[:, 0:HALVES])
+                nc.vector.tensor_sub(
+                    out=shift[:], in0=norm_cols[:, 2 * HALVES : 3 * HALVES], in1=shift[:]
+                )
+
+            def normalise_scalars(c):
+                if c >= CHUNKS:
+                    return
                 cols = slice(c * CHUNK, (c + 1) * CHUNK)
                 for h in range(HALVES):
                     nc.vector.tensor_scalar(
@@ -327,46 +443,46 @@ def tile_feedforward_pb_t_kernel(
                         op0=MULT,
                         op1=ADD,
                     )
-                for h in range(HALVES):
-                    nc.vector.tensor_scalar(
-                        out=y[:, 2 + h : BLOCKS : 2, cols],
-                        in0=y[:, 2 + h : BLOCKS : 2, cols],
-                        scalar1=gain[:, HALVES + h : HALVES + h + 1],
-                        scalar2=None,
-                        op0=MULT,
-                    )
 
-            def store_pair(first_tile):
-                result = rows_out.tile([P, 2, GROUPS * OUT], F32, name="result")
-                scalars_t = scalar_psum.tile([P, 2, OUT], F32, name="scalars_t")
-                for i in range(2):
-                    nodes = slice((first_tile + i) * P, (first_tile + i + 1) * P)
-                    for h in range(HALVES):
-                        nc.tensor.transpose(
-                            scalars_t[:, i, h * P : (h + 1) * P], y[:, h, nodes], ident_f32[:]
-                        )
-                nc.vector.tensor_copy(out=result[:, :, 0:OUT], in_=scalars_t[:])
-                for i in range(2):
-                    nodes = slice((first_tile + i) * P, (first_tile + i + 1) * P)
-                    for h in range(HALVES):
-                        vectors_t = vector_psum.tile([P, DV, P], F32, name="vectors_t")
-                        for d in range(DV):
+            def store_scalars(c, free_banks):
+                rows = rows_out.tile([P, CHUNK_TILES, OUT], F32, name="scalar_rows")
+                for i in range(0, CHUNK_TILES, 2):
+                    scalars_t = next_bank(free_banks, [P, 2, OUT])
+                    for t in range(2):
+                        nodes = slice((c * CHUNK_TILES + i + t) * P, (c * CHUNK_TILES + i + t + 1) * P)
+                        for h in range(HALVES):
                             nc.tensor.transpose(
-                                vectors_t[:, d, :], y[:, 2 * (1 + d) + h, nodes], ident_f32[:]
+                                scalars_t[:, t, h * P : (h + 1) * P], y[:, h, nodes], ident_f32[:]
                             )
-                        start = OUT + h * DV * P
-                        nc.scalar.copy(
-                            out=result[:, i, start : start + DV * P].rearrange(
-                                "p (o d) -> p o d", d=DV
-                            ),
-                            in_=vectors_t[:].rearrange("p d o -> p o d"),
-                        )
-                nc.sync.dma_start(out=out_tiles[:, first_tile : first_tile + 2, :], in_=result[:])
+                    nc.scalar.copy(out=rows[:, i : i + 2, :], in_=scalars_t[:])
+                tiles = slice(c * CHUNK_TILES, (c + 1) * CHUNK_TILES)
+                nc.sync.dma_start(out=out_tiles[:, tiles, 0:OUT], in_=rows[:])
+
+            def storer(pair, free_banks):
+                return lambda: store_vectors(pair, free_banks)
 
             with tc.manual_schedule():
-                normalise_chunk(0)
+                first_store = VECTOR_STEPS + 2
+                for now in range(LAST_VECTOR_INPUT, STEPS):
+                    if now == VECTOR_STEPS:
+                        iteration(now, (nothing, nothing, nothing, vector_spread))
+                    elif now == VECTOR_STEPS + 1:
+                        iteration(now, (vector_root, vector_gain, flip_gain, spread_gain))
+                    elif now >= first_store:
+                        free_banks = (2, 5, 7) if now + FLIP_LEAD < STEPS else (2, 5, 7, 0, 1)
+                        pair = 2 * (now - first_store)
+                        iteration(
+                            now, (storer(pair, free_banks), nothing, storer(pair + 1, free_banks), nothing)
+                        )
+                    else:
+                        iteration(now)
+                scalar_gain()
+                all_banks = (0, 1, 2, 3, 4, 5, 6, 7)
+                left = list(range(2 * (STEPS - first_store), PAIRS))
+                normalise_scalars(0)
                 for c in range(CHUNKS):
-                    store_pair(c * CHUNK_TILES)
-                    if c + 1 < CHUNKS:
-                        normalise_chunk(c + 1)
-                    store_pair(c * CHUNK_TILES + 2)
+                    normalise_scalars(c + 1)
+                    if c % 2 == 0 and left:
+                        store_vectors(left[0], all_banks)
+                        left.remove(left[0])
+                    store_scalars(c, all_banks)

@@ -66,7 +66,7 @@ def tile_feedforward_pb_t_kernel(
         grouping = whole.enter_context(tc.tile_pool(name="grouping", bufs=2))
         quantised = whole.enter_context(tc.tile_pool(name="quantised", bufs=FLIP_LEAD + 1))
         bypass_in = whole.enter_context(tc.tile_pool(name="bypass_in", bufs=2))
-        sums = whole.enter_context(tc.tile_pool(name="sums", bufs=3))
+        sums = whole.enter_context(tc.tile_pool(name="sums", bufs=5))
         scrap = whole.enter_context(tc.tile_pool(name="scrap", bufs=2))
         banks = whole.enter_context(tc.psum_pool(name="banks", bufs=1))
 
@@ -89,6 +89,7 @@ def tile_feedforward_pb_t_kernel(
         f_cols_of = {}
         operand_of = {}
         product_of = {}
+        bypass_of = {}
 
         def place(s):
             if s < VECTOR_STEPS:
@@ -112,7 +113,13 @@ def tile_feedforward_pb_t_kernel(
                     return
                 tiles = slice(c * CHUNK_TILES, (c + 1) * CHUNK_TILES)
                 x_vectors = loads.tile([P, CHUNK_TILES, DV * HID], BF16, name="x_vectors")
-                nc.sync.dma_start(out=x_vectors[:], in_=h2_tiles[:, tiles, HID:])
+                pieces = 2 if c == 0 else 1
+                width = CHUNK_TILES // pieces
+                for piece in range(pieces):
+                    nc.sync.dma_start(
+                        out=x_vectors[:, piece * width : (piece + 1) * width, :],
+                        in_=h2_tiles[:, tiles.start + piece * width : tiles.start + (piece + 1) * width, HID:],
+                    )
                 x_vectors_of[c] = x_vectors
 
             def load_features(c):
@@ -171,10 +178,14 @@ def tile_feedforward_pb_t_kernel(
                     return
                 picked = sorting.tile([P, 2, CHUNK, 2], BF16, name="picked")
                 by_q = x_vectors_of[c][:].rearrange("p t (q r) -> p (t q) r", r=4 * DV)
-                nc.vector.tensor_copy(
-                    out=picked[:],
-                    in_=by_q.rearrange("p m (u e d) -> p d u m e", u=2, e=2, d=DV)[:, g - 1],
-                )
+                component = by_q.rearrange("p m (u e d) -> p d u m e", u=2, e=2, d=DV)[:, g - 1]
+                pieces = 2 if c == 0 else 1
+                width = CHUNK // pieces
+                for piece in range(pieces):
+                    nc.vector.tensor_copy(
+                        out=picked[:, :, piece * width : (piece + 1) * width, :],
+                        in_=component[:, :, piece * width : (piece + 1) * width, :],
+                    )
                 picked_of[s] = picked
                 if g == DV:
                     load_vectors(c + 2)
@@ -198,7 +209,7 @@ def tile_feedforward_pb_t_kernel(
                     return
                 if g == 1:
                     f_cols_of[c] = bypass_in.tile([P, DV, CHUNK], BF16, name="f_cols")
-                    nc.vector.tensor_copy(out=f_cols_scalar[:, c, :], in_=f_flipped[:, 0, :])
+                    nc.scalar.copy(out=f_cols_scalar[:, c, :], in_=f_flipped[:, 0, :])
                     nc.vector.tensor_copy(out=f_cols_of[c][:, 0, :], in_=f_flipped[:, 1, :])
                 if g == DV:
                     nc.vector.tensor_copy(out=f_cols_of[c][:, 1:DV, :], in_=f_flipped[:])
@@ -250,6 +261,11 @@ def tile_feedforward_pb_t_kernel(
                     start=True,
                     stop=True,
                 )
+                product_of[(s, h)] = mx_acc
+
+            def bypass_half(s, h):
+                c, g = place(s)
+                w = min(g, 1)
                 byp_acc = bank(6 + h if g > 0 else 6, [P, CHUNK], F32)
                 nc.tensor.matmul(
                     byp_acc[:],
@@ -260,11 +276,11 @@ def tile_feedforward_pb_t_kernel(
                 )
                 bypass = sums.tile([P, CHUNK], F32, name="bypass")
                 nc.scalar.mul(out=bypass[:], in_=byp_acc[:], mul=1.0 / math.sqrt(BYP))
-                product_of[(s, h)] = (mx_acc, bypass)
+                bypass_of[(s, h)] = bypass
 
             def add_half(s, h):
                 c, g = place(s)
-                mx_acc, bypass = product_of[(s, h)]
+                mx_acc, bypass = product_of[(s, h)], bypass_of[(s, h)]
                 nc.vector.scalar_tensor_tensor(
                     out=y[:, 2 * g + h, c * CHUNK : (c + 1) * CHUNK],
                     in0=mx_acc[:],
@@ -300,12 +316,14 @@ def tile_feedforward_pb_t_kernel(
                 run(sort_step, now + SORT_LEAD)
                 run(flip_half, now + FLIP_LEAD, 0)
                 run(multiply_half, now, 0)
+                run(bypass_half, now + 1, 0)
                 between[0]()
                 run(flip_half, now + FLIP_LEAD, 1)
                 run(quantise_step, now + FLIP_LEAD - 1)
                 run(add_half, now, 0)
                 between[1]()
                 run(multiply_half, now, 1)
+                run(bypass_half, now + 1, 1)
                 between[2]()
                 run(add_half, now, 1)
                 if now - 1 < VECTOR_STEPS:
@@ -386,6 +404,19 @@ def tile_feedforward_pb_t_kernel(
                     op0=MULT,
                     op1=ADD,
                 )
+                for tile in (2 * pair, 2 * pair + 1):
+                    if early_after_all(tile):
+                        nc.gpsimd.tensor_scalar(
+                            out=y[:, 2 + LATE : BLOCKS : 2, tile * P : (tile + 1) * P],
+                            in0=y[:, 2 + LATE : BLOCKS : 2, tile * P : (tile + 1) * P],
+                            scalar1=gain[:, HALVES + LATE : HALVES + LATE + 1],
+                            scalar2=0.0,
+                            op0=MULT,
+                            op1=ADD,
+                        )
+
+            def early_after_all(tile):
+                return tile % 4 == 3
 
             def store_vectors(pair, free_banks):
                 normalise_pair(pair + 2)
@@ -401,7 +432,7 @@ def tile_feedforward_pb_t_kernel(
                         part = rows[:, i, h * DV * P : (h + 1) * DV * P].rearrange(
                             "p (o d) -> p o d", d=DV
                         )
-                        if h == LATE:
+                        if h == LATE and not early_after_all(2 * pair + i):
                             nc.vector.tensor_tensor(
                                 out=part,
                                 in0=vectors_t[:].rearrange("p d o -> p o d"),

@@ -494,6 +494,7 @@ def tile_feedforward_pb_t_kernel(
 
             with tc.manual_schedule():
                 first_store = VECTOR_STEPS + 2
+                stored = 0
                 for now in range(LAST_VECTOR_INPUT, STEPS):
                     if now == VECTOR_STEPS:
                         iteration(now, (nothing, nothing, nothing, vector_spread))
@@ -501,15 +502,15 @@ def tile_feedforward_pb_t_kernel(
                         iteration(now, (vector_root, vector_gain, flip_gain, spread_gain))
                     elif now >= first_store:
                         free_banks = (2, 5, 7) if now + FLIP_LEAD < STEPS else (2, 5, 7, 0, 1)
-                        pair = 2 * (now - first_store)
-                        iteration(
-                            now, (storer(pair, free_banks), nothing, storer(pair + 1, free_banks), nothing)
-                        )
+                        woven = 2 if now < STEPS - 2 else 3
+                        pairs = [storer(stored + i, free_banks) for i in range(woven)] + [nothing]
+                        stored = stored + woven
+                        iteration(now, (pairs[0], nothing, pairs[1], pairs[2]))
                     else:
                         iteration(now)
                 scalar_gain()
                 all_banks = (0, 1, 2, 3, 4, 5, 6, 7)
-                left = list(range(2 * (STEPS - first_store), PAIRS))
+                left = list(range(stored, PAIRS))
                 normalise_scalars(0)
                 for c in range(CHUNKS):
                     normalise_scalars(c + 1)

@@ -210,7 +210,7 @@ def tile_feedforward_pb_t_kernel(
                 if g == 1:
                     f_cols_of[c] = bypass_in.tile([P, DV, CHUNK], BF16, name="f_cols")
                     nc.scalar.copy(out=f_cols_scalar[:, c, :], in_=f_flipped[:, 0, :])
-                    nc.vector.tensor_copy(out=f_cols_of[c][:, 0, :], in_=f_flipped[:, 1, :])
+                    nc.scalar.copy(out=f_cols_of[c][:, 0, :], in_=f_flipped[:, 1, :])
                 if g == DV:
                     nc.vector.tensor_copy(out=f_cols_of[c][:, 1:DV, :], in_=f_flipped[:])
                     load_features(c + 2)

@@ -36,6 +36,8 @@ LAST_VECTOR_INPUT = VECTOR_STEPS - FLIP_LEAD
 LATE = 1
 EARLY = 1 - LATE
 PAIRS = NODE_TILES // 2
+TAIL_PAIRS = 2
+FIRST_TAIL_PAIR = PAIRS - TAIL_PAIRS
 EPS = 1e-5
 
 FLOPS = 2 * NODES * GROUPS * OUT * (HID + BYP)
@@ -178,13 +180,14 @@ def tile_feedforward_pb_t_kernel(
                     return
                 picked = sorting.tile([P, 2, CHUNK, 2], BF16, name="picked")
                 by_q = x_vectors_of[c][:].rearrange("p t (q r) -> p (t q) r", r=4 * DV)
-                component = by_q.rearrange("p m (u e d) -> p d u m e", u=2, e=2, d=DV)[:, g - 1]
+                component = by_q.rearrange("p m (u e d) -> p d m u e", u=2, e=2, d=DV)[:, g - 1]
+                in_order = picked[:].rearrange("p u m e -> p m u e")
                 pieces = 2 if c == 0 else 1
                 width = CHUNK // pieces
                 for piece in range(pieces):
                     nc.vector.tensor_copy(
-                        out=picked[:, :, piece * width : (piece + 1) * width, :],
-                        in_=component[:, :, piece * width : (piece + 1) * width, :],
+                        out=in_order[:, piece * width : (piece + 1) * width],
+                        in_=component[:, piece * width : (piece + 1) * width],
                     )
                 picked_of[s] = picked
                 if g == DV:
@@ -416,7 +419,7 @@ def tile_feedforward_pb_t_kernel(
                         )
 
             def early_after_all(tile):
-                return tile % 4 == 3
+                return tile % 4 == 3 or tile >= 2 * FIRST_TAIL_PAIR
 
             def store_vectors(pair, free_banks):
                 normalise_pair(pair + 2)
@@ -485,7 +488,8 @@ def tile_feedforward_pb_t_kernel(
                             nc.tensor.transpose(
                                 scalars_t[:, t, h * P : (h + 1) * P], y[:, h, nodes], ident_f32[:]
                             )
-                    nc.scalar.copy(out=rows[:, i : i + 2, :], in_=scalars_t[:])
+                    copy_out = nc.scalar.copy if i == 0 else nc.vector.tensor_copy
+                    copy_out(out=rows[:, i : i + 2, :], in_=scalars_t[:])
                 tiles = slice(c * CHUNK_TILES, (c + 1) * CHUNK_TILES)
                 nc.sync.dma_start(out=out_tiles[:, tiles, 0:OUT], in_=rows[:])
 
@@ -508,13 +512,12 @@ def tile_feedforward_pb_t_kernel(
                         iteration(now, (pairs[0], nothing, pairs[1], pairs[2]))
                     else:
                         iteration(now)
+                store_vectors(stored, (2, 5, 7, 0, 1))
                 scalar_gain()
+                for pair in range(stored + 1, PAIRS):
+                    store_vectors(pair, (2, 5, 7, 0, 1))
                 all_banks = (0, 1, 2, 3, 4, 5, 6, 7)
-                left = list(range(stored, PAIRS))
                 normalise_scalars(0)
                 for c in range(CHUNKS):
                     normalise_scalars(c + 1)
-                    if c % 2 == 0 and left:
-                        store_vectors(left[0], all_banks)
-                        left.remove(left[0])
                     store_scalars(c, all_banks)

@@ -30,8 +30,8 @@ HALVES = OUT // P
 BLOCKS = GROUPS * HALVES
 VECTOR_STEPS = CHUNKS * DV
 STEPS = VECTOR_STEPS + CHUNKS
-FLIP_LEAD = 4
-SORT_LEAD = FLIP_LEAD + 2
+FLIP_LEAD = 3
+SORT_LEAD = FLIP_LEAD + 1
 LAST_VECTOR_INPUT = VECTOR_STEPS - FLIP_LEAD
 LATE = 1
 EARLY = 1 - LATE
@@ -134,6 +134,9 @@ def tile_feedforward_pb_t_kernel(
 
             load_vectors(0)
             load_features(0)
+            byp_w = keep.tile([P, 2, OUT], BF16)
+            nc.sync.dma_start(out=byp_w[:, 1, :], in_=byp_W1)
+            load_vectors(1)
 
             ident_f32 = keep.tile([P, P], F32)
             make_identity(nc, ident_f32[:])
@@ -147,32 +150,30 @@ def tile_feedforward_pb_t_kernel(
             w_words = keep.tile([P, 2, 2 * OUT], U8, align_bytes=64)
             w_planes = keep.tile([P, 2, OUT], U8, align_bytes=64)
             nc.vector.memset(w_planes[:].rearrange("p w n -> p (w n)").bitcast(I32), 0)
-            for w, (words, scales) in enumerate(
-                ((lin3_W0_words, lin3_W0_scales), (lin3_W1_words, lin3_W1_scales))
-            ):
+            weights = ((lin3_W0_words, lin3_W0_scales), (lin3_W1_words, lin3_W1_scales))
+
+            def load_weights(w):
+                words, scales = weights[w]
                 nc.sync.dma_start(out=w_words[:, w, :].bitcast(I32), in_=words[0].bitcast(I32))
                 for quadrant in range(4):
                     nc.sync.dma_start(
                         out=w_planes[32 * quadrant : 32 * quadrant + 4, w, :].bitcast(I32),
                         in_=scales[0, 4 * quadrant : 4 * quadrant + 4, :].bitcast(I32),
                     )
-            byp_w = keep.tile([P, 2, OUT], BF16)
+
+            load_weights(1)
+
+            load_features(1)
+            load_weights(0)
             nc.sync.dma_start(out=byp_w[:, 0, :], in_=byp_W0)
-            nc.sync.dma_start(out=byp_w[:, 1, :], in_=byp_W1)
+            load_scalars(0)
+            load_scalars(1)
 
             norm_rows = keep.tile([P, P], BF16)
             nc.vector.memset(norm_rows[:], 0.0)
             nc.sync.dma_start(out=norm_rows[0:4, :], in_=bn_weight.rearrange("(r c) -> r c", c=P))
             nc.sync.dma_start(out=norm_rows[4:6, :], in_=bn_bias.rearrange("(r c) -> r c", c=P))
-            norm_flipped = bank(2, [P, P], BF16)
-            nc.tensor.transpose(norm_flipped[:], norm_rows[:], ident_bf16[:])
             norm_cols = keep.tile([P, 8], F32)
-            nc.vector.tensor_copy(out=norm_cols[:], in_=norm_flipped[:, 0:8])
-
-            load_vectors(1)
-            load_features(1)
-            load_scalars(0)
-            load_scalars(1)
 
             def sort_step(s):
                 c, g = place(s)
@@ -218,6 +219,9 @@ def tile_feedforward_pb_t_kernel(
                     nc.vector.tensor_copy(out=f_cols_of[c][:, 1:DV, :], in_=f_flipped[:])
                     load_features(c + 2)
 
+            def sorting_done(s):
+                return VECTOR_STEPS - SORT_LEAD <= s - FLIP_LEAD < VECTOR_STEPS
+
             def flip_half(s, half):
                 c, g = place(s)
                 flipped = bank(half, [P, 2, 2, P], F32)
@@ -231,7 +235,8 @@ def tile_feedforward_pb_t_kernel(
                         nc.tensor.transpose(flipped[:, u, t - 2 * half, :], words, ident_f32[:])
                 if half == 0:
                     grouped_of[s] = grouping.tile([P, CHUNK, 2], F32, name="grouped", align_bytes=64)
-                nc.scalar.copy(
+                copy_out = nc.vector.tensor_copy if sorting_done(s) else nc.scalar.copy
+                copy_out(
                     out=grouped_of[s][:, half * 2 * P : (half + 1) * 2 * P, :],
                     in_=flipped[:].rearrange("p u i n -> p (i n) u"),
                 )
@@ -352,6 +357,14 @@ def tile_feedforward_pb_t_kernel(
             gain_square = keep.tile([P, P], F32)
             gain_rows = keep.tile([P, P, DV], F32)
             mean_var = keep.tile([P, HALVES, 2], F32)
+
+            def flip_norm():
+                norm_flipped = bank(2, [P, P], BF16)
+                nc.tensor.transpose(norm_flipped[:], norm_rows[:], ident_bf16[:])
+                product_of["norm"] = norm_flipped
+
+            def keep_norm():
+                nc.vector.tensor_copy(out=norm_cols[:], in_=product_of["norm"][:, 0:8])
 
             def vector_spread():
                 nc.vector.tensor_reduce(
@@ -500,7 +513,9 @@ def tile_feedforward_pb_t_kernel(
                 first_store = VECTOR_STEPS + 2
                 stored = 0
                 for now in range(LAST_VECTOR_INPUT, STEPS):
-                    if now == VECTOR_STEPS:
+                    if now == LAST_VECTOR_INPUT:
+                        iteration(now, (flip_norm, nothing, keep_norm, nothing))
+                    elif now == VECTOR_STEPS:
                         iteration(now, (nothing, nothing, nothing, vector_spread))
                     elif now == VECTOR_STEPS + 1:
                         iteration(now, (vector_root, vector_gain, flip_gain, spread_gain))

@@ -29,13 +29,17 @@ OUT = 256
 HALVES = OUT // P
 BLOCKS = GROUPS * HALVES
 VECTOR_STEPS = CHUNKS * DV
-STEPS = VECTOR_STEPS + CHUNKS
+PAUSE = 1
+STEPS = VECTOR_STEPS + PAUSE + CHUNKS
+LAST_VECTOR_STEP = VECTOR_STEPS - 1
 FLIP_LEAD = 3
 SORT_LEAD = FLIP_LEAD + 1
+FIRST_STORE = VECTOR_STEPS + 2
 LAST_VECTOR_INPUT = VECTOR_STEPS - FLIP_LEAD
 LATE = 1
 EARLY = 1 - LATE
 PAIRS = NODE_TILES // 2
+SCALARS_AHEAD = 4
 TAIL_PAIRS = 2
 FIRST_TAIL_PAIR = PAIRS - TAIL_PAIRS
 EPS = 1e-5
@@ -64,7 +68,7 @@ def tile_feedforward_pb_t_kernel(
 
     with ExitStack() as whole:
         keep = whole.enter_context(tc.tile_pool(name="keep", bufs=1))
-        scalar_in = whole.enter_context(tc.tile_pool(name="scalar_in", bufs=2))
+        scalar_in = whole.enter_context(tc.tile_pool(name="scalar_in", bufs=SCALARS_AHEAD))
         grouping = whole.enter_context(tc.tile_pool(name="grouping", bufs=2))
         quantised = whole.enter_context(tc.tile_pool(name="quantised", bufs=FLIP_LEAD + 1))
         bypass_in = whole.enter_context(tc.tile_pool(name="bypass_in", bufs=2))
@@ -96,7 +100,7 @@ def tile_feedforward_pb_t_kernel(
         def place(s):
             if s < VECTOR_STEPS:
                 return s // DV, 1 + s % DV
-            return s - VECTOR_STEPS, 0
+            return s - VECTOR_STEPS - PAUSE, 0
 
         def load_scalars(c):
             if c >= CHUNKS:
@@ -108,7 +112,7 @@ def tile_feedforward_pb_t_kernel(
 
         with ExitStack() as vector_input:
             loads = vector_input.enter_context(tc.tile_pool(name="loads", bufs=2))
-            sorting = vector_input.enter_context(tc.tile_pool(name="sorting", bufs=DV))
+            sorting = vector_input.enter_context(tc.tile_pool(name="sorting", bufs=2))
 
             def load_vectors(c):
                 if c >= CHUNKS:
@@ -166,8 +170,8 @@ def tile_feedforward_pb_t_kernel(
             load_features(1)
             load_weights(0)
             nc.sync.dma_start(out=byp_w[:, 0, :], in_=byp_W0)
-            load_scalars(0)
-            load_scalars(1)
+            for c in range(SCALARS_AHEAD):
+                load_scalars(c)
 
             norm_rows = keep.tile([P, P], BF16)
             nc.vector.memset(norm_rows[:], 0.0)
@@ -224,7 +228,7 @@ def tile_feedforward_pb_t_kernel(
 
             def flip_half(s, half):
                 c, g = place(s)
-                flipped = bank(half, [P, 2, 2, P], F32)
+                flipped = bank(half if s < FIRST_STORE + FLIP_LEAD else 0, [P, 2, 2, P], F32)
                 for u in range(2):
                     for t in range(2 * half, 2 * half + 2):
                         if g == 0:
@@ -243,7 +247,7 @@ def tile_feedforward_pb_t_kernel(
                 if g > 0:
                     flip_features(s, half)
                 elif half == 1:
-                    load_scalars(c + 2)
+                    load_scalars(c + SCALARS_AHEAD)
 
             def quantise_step(s):
                 codes = quantised.tile([P, CHUNK], U32, name="codes", align_bytes=64)
@@ -314,7 +318,7 @@ def tile_feedforward_pb_t_kernel(
                         )
 
             def run(stage, s, *part):
-                if 0 <= s < STEPS:
+                if 0 <= s < VECTOR_STEPS or VECTOR_STEPS + PAUSE <= s < STEPS:
                     stage(s, *part)
 
             def nothing():
@@ -334,7 +338,7 @@ def tile_feedforward_pb_t_kernel(
                 run(bypass_half, now + 1, 1)
                 between[2]()
                 run(add_half, now, 1)
-                if now - 1 < VECTOR_STEPS:
+                if now - 1 < LAST_VECTOR_STEP:
                     run(measure_step, now - 1)
                 if now >= VECTOR_STEPS:
                     run(measure_step, now)
@@ -345,7 +349,7 @@ def tile_feedforward_pb_t_kernel(
                     iteration(now)
 
         with ExitStack() as storing:
-            rows_out = storing.enter_context(tc.tile_pool(name="rows_out", bufs=3))
+            rows_out = storing.enter_context(tc.tile_pool(name="rows_out", bufs=4))
             turn = {"bank": 0}
 
             def next_bank(free_banks, shape):
@@ -366,6 +370,9 @@ def tile_feedforward_pb_t_kernel(
             def keep_norm():
                 nc.vector.tensor_copy(out=norm_cols[:], in_=product_of["norm"][:, 0:8])
 
+            def measure_last():
+                measure_step(LAST_VECTOR_STEP)
+
             def vector_spread():
                 nc.vector.tensor_reduce(
                     out=vector_sum[:],
@@ -381,8 +388,6 @@ def tile_feedforward_pb_t_kernel(
                     op0=MULT,
                     op1=ADD,
                 )
-
-            def vector_root():
                 nc.scalar.sqrt(out=spread[:, HALVES:], in_=spread[:, HALVES:])
 
             def vector_gain():
@@ -510,19 +515,18 @@ def tile_feedforward_pb_t_kernel(
                 return lambda: store_vectors(pair, free_banks)
 
             with tc.manual_schedule():
-                first_store = VECTOR_STEPS + 2
-                stored = 0
+                stored = 1
                 for now in range(LAST_VECTOR_INPUT, STEPS):
                     if now == LAST_VECTOR_INPUT:
                         iteration(now, (flip_norm, nothing, keep_norm, nothing))
                     elif now == VECTOR_STEPS:
-                        iteration(now, (nothing, nothing, nothing, vector_spread))
+                        iteration(now, (measure_last, nothing, vector_spread, vector_gain))
                     elif now == VECTOR_STEPS + 1:
-                        iteration(now, (vector_root, vector_gain, flip_gain, spread_gain))
-                    elif now >= first_store:
-                        free_banks = (2, 5, 7) if now + FLIP_LEAD < STEPS else (2, 5, 7, 0, 1)
-                        woven = 2 if now < STEPS - 2 else 3
-                        pairs = [storer(stored + i, free_banks) for i in range(woven)] + [nothing]
+                        iteration(now, (flip_gain, spread_gain, storer(0, (2, 5, 7)), nothing))
+                    elif now >= FIRST_STORE:
+                        free_banks = (2, 5, 7, 1) if now + FLIP_LEAD < STEPS else (2, 5, 7, 0, 1)
+                        woven = 2 if now < STEPS - 1 else 1
+                        pairs = [storer(stored + i, free_banks) for i in range(woven)] + [nothing, nothing]
                         stored = stored + woven
                         iteration(now, (pairs[0], nothing, pairs[1], pairs[2]))
                     else:

@@ -218,7 +218,7 @@ def tile_feedforward_pb_t_kernel(
                 if g == 1:
                     f_cols_of[c] = bypass_in.tile([P, DV, CHUNK], BF16, name="f_cols")
                     nc.scalar.copy(out=f_cols_scalar[:, c, :], in_=f_flipped[:, 0, :])
-                    nc.scalar.copy(out=f_cols_of[c][:, 0, :], in_=f_flipped[:, 1, :])
+                    nc.vector.tensor_copy(out=f_cols_of[c][:, 0, :], in_=f_flipped[:, 1, :])
                 if g == DV:
                     nc.vector.tensor_copy(out=f_cols_of[c][:, 1:DV, :], in_=f_flipped[:])
                     load_features(c + 2)

@@ -13,7 +13,9 @@ FP8X4 = mybir.dt.float8_e4m3fn_x4
 FP4X4 = mybir.dt.float4_e2m1fn_x4
 ADD = mybir.AluOpType.add
 MULT = mybir.AluOpType.mult
+SUBTRACT = mybir.AluOpType.subtract
 SQUARE = mybir.ActivationFunctionType.Square
+SQRT = mybir.ActivationFunctionType.Sqrt
 
 P = 128
 NODES = 4096
@@ -150,6 +152,8 @@ def tile_feedforward_pb_t_kernel(
             warm = keep.tile([P, 1], F32)
             nc.vector.memset(warm[:], 1.0)
             nc.scalar.sqrt(out=warm[:], in_=warm[:])
+            eps = keep.tile([P, 1], F32)
+            nc.vector.memset(eps[:], EPS)
 
             w_words = keep.tile([P, 2, 2 * OUT], U8, align_bytes=64)
             w_planes = keep.tile([P, 2, OUT], U8, align_bytes=64)
@@ -349,7 +353,8 @@ def tile_feedforward_pb_t_kernel(
                     iteration(now)
 
         with ExitStack() as storing:
-            rows_out = storing.enter_context(tc.tile_pool(name="rows_out", bufs=4))
+            rows_out = storing.enter_context(tc.tile_pool(name="rows_out", bufs=7))
+            gain_copies = storing.enter_context(tc.tile_pool(name="gain_copies", bufs=2))
             turn = {"bank": 0}
 
             def next_bank(free_banks, shape):
@@ -380,15 +385,13 @@ def tile_feedforward_pb_t_kernel(
                     axis=mybir.AxisListType.X,
                     op=ADD,
                 )
-                nc.vector.tensor_scalar(
+                nc.scalar.activation(
                     out=spread[:, HALVES:],
-                    in0=vector_sum[:],
-                    scalar1=1.0 / (DV * NODES),
-                    scalar2=EPS,
-                    op0=MULT,
-                    op1=ADD,
+                    in_=vector_sum[:],
+                    func=SQRT,
+                    scale=1.0 / (DV * NODES),
+                    bias=eps[:],
                 )
-                nc.scalar.sqrt(out=spread[:, HALVES:], in_=spread[:, HALVES:])
 
             def vector_gain():
                 nc.vector.reciprocal(out=gain[:, HALVES:], in_=spread[:, HALVES:])
@@ -399,8 +402,7 @@ def tile_feedforward_pb_t_kernel(
                     out=gain_square[:],
                     in_=gain[:, HALVES + LATE : HALVES + LATE + 1].to_broadcast([P, P]),
                 )
-                normalise_pair(0)
-                normalise_pair(1)
+                normalise_pairs((0,))
 
             def flip_gain():
                 gain_flipped = bank(5, [P, P], F32)
@@ -413,14 +415,18 @@ def tile_feedforward_pb_t_kernel(
                     in_=product_of["gain"][:].unsqueeze(2).to_broadcast([P, P, DV]),
                 )
 
-            def normalise_pair(pair):
-                if pair >= PAIRS:
-                    return
+            def normalise_pairs(pairs):
+                now_gain = gain_copies.tile([P, HALVES], F32, name="now_gain")
+                nc.vector.tensor_copy(out=now_gain[:], in_=gain[:, HALVES:])
+                for pair in pairs:
+                    normalise_pair(pair, now_gain)
+
+            def normalise_pair(pair, now_gain):
                 cols = slice(2 * pair * P, 2 * (pair + 1) * P)
                 nc.gpsimd.tensor_scalar(
                     out=y[:, 2 + EARLY : BLOCKS : 2, cols],
                     in0=y[:, 2 + EARLY : BLOCKS : 2, cols],
-                    scalar1=gain[:, HALVES + EARLY : HALVES + EARLY + 1],
+                    scalar1=now_gain[:, EARLY : EARLY + 1],
                     scalar2=0.0,
                     op0=MULT,
                     op1=ADD,
@@ -430,7 +436,7 @@ def tile_feedforward_pb_t_kernel(
                         nc.gpsimd.tensor_scalar(
                             out=y[:, 2 + LATE : BLOCKS : 2, tile * P : (tile + 1) * P],
                             in0=y[:, 2 + LATE : BLOCKS : 2, tile * P : (tile + 1) * P],
-                            scalar1=gain[:, HALVES + LATE : HALVES + LATE + 1],
+                            scalar1=now_gain[:, LATE : LATE + 1],
                             scalar2=0.0,
                             op0=MULT,
                             op1=ADD,
@@ -440,8 +446,7 @@ def tile_feedforward_pb_t_kernel(
                 return tile % 4 == 3 or tile >= 2 * FIRST_TAIL_PAIR
 
             def store_vectors(pair, free_banks):
-                normalise_pair(pair + 2)
-                rows = rows_out.tile([P, 2, DV * OUT], F32, name="vector_rows")
+                rows = rows_out.tile([P, 2, DV * OUT], F32, name="rows")
                 for i in range(2):
                     nodes = slice((2 * pair + i) * P, (2 * pair + i + 1) * P)
                     for h in (LATE, EARLY):
@@ -469,18 +474,22 @@ def tile_feedforward_pb_t_kernel(
                     nc.vector.bn_aggr(
                         out=mean_var[:, h, :], in_=scalar_stats[:, h].rearrange("p c s -> p (c s)")
                     )
-                nc.vector.tensor_scalar(
-                    out=spread[:, 0:HALVES], in0=mean_var[:, :, 1], scalar1=EPS, scalar2=None, op0=ADD
+                nc.scalar.activation(
+                    out=spread[:, 0:HALVES], in_=mean_var[:, :, 1], func=SQRT, bias=eps[:]
                 )
-                nc.scalar.sqrt(out=spread[:, 0:HALVES], in_=spread[:, 0:HALVES])
                 nc.vector.reciprocal(out=gain[:, 0:HALVES], in_=spread[:, 0:HALVES])
                 nc.vector.tensor_mul(
                     out=gain[:, 0:HALVES], in0=gain[:, 0:HALVES], in1=norm_cols[:, 0:HALVES]
                 )
-                nc.vector.tensor_mul(out=shift[:], in0=mean_var[:, :, 0], in1=gain[:, 0:HALVES])
-                nc.vector.tensor_sub(
-                    out=shift[:], in0=norm_cols[:, 2 * HALVES : 3 * HALVES], in1=shift[:]
-                )
+                for h in range(HALVES):
+                    nc.vector.scalar_tensor_tensor(
+                        out=shift[:, h : h + 1],
+                        in0=mean_var[:, h, 0:1],
+                        scalar=gain[:, h : h + 1],
+                        in1=norm_cols[:, 2 * HALVES + h : 2 * HALVES + h + 1],
+                        op0=MULT,
+                        op1=SUBTRACT,
+                    )
 
             def normalise_scalars(c):
                 if c >= CHUNKS:
@@ -493,11 +502,11 @@ def tile_feedforward_pb_t_kernel(
                         scalar1=gain[:, h : h + 1],
                         scalar2=shift[:, h : h + 1],
                         op0=MULT,
-                        op1=ADD,
+                        op1=SUBTRACT,
                     )
 
             def store_scalars(c, free_banks):
-                rows = rows_out.tile([P, CHUNK_TILES, OUT], F32, name="scalar_rows")
+                rows = rows_out.tile([P, CHUNK_TILES, OUT], F32, name="rows")
                 for i in range(0, CHUNK_TILES, 2):
                     scalars_t = next_bank(free_banks, [P, 2, OUT])
                     for t in range(2):
@@ -514,26 +523,40 @@ def tile_feedforward_pb_t_kernel(
             def storer(pair, free_banks):
                 return lambda: store_vectors(pair, free_banks)
 
+            def pairs_of_turn(now):
+                first = max(0, 2 * (now - FIRST_STORE) + 1)
+                if now == STEPS:
+                    return range(FIRST_TAIL_PAIR, PAIRS)
+                return range(first, min(2 * (now - FIRST_STORE) + 3, FIRST_TAIL_PAIR))
+
+            def normalise_ahead(now):
+                first = 2 * (now - FIRST_STORE) + 4 if now >= FIRST_STORE else 1
+                normalise_pairs(range(first, min(2 * (now - FIRST_STORE) + 6, PAIRS)))
+
+            def normaliser(now):
+                return lambda: normalise_ahead(now)
+
+            def spread_and_normalise():
+                spread_gain()
+                normalise_ahead(FIRST_STORE - 1)
+
             with tc.manual_schedule():
-                stored = 1
                 for now in range(LAST_VECTOR_INPUT, STEPS):
                     if now == LAST_VECTOR_INPUT:
                         iteration(now, (flip_norm, nothing, keep_norm, nothing))
                     elif now == VECTOR_STEPS:
                         iteration(now, (measure_last, nothing, vector_spread, vector_gain))
                     elif now == VECTOR_STEPS + 1:
-                        iteration(now, (flip_gain, spread_gain, storer(0, (2, 5, 7)), nothing))
+                        iteration(now, (flip_gain, spread_and_normalise, storer(0, (2, 5, 7)), nothing))
                     elif now >= FIRST_STORE:
                         free_banks = (2, 5, 7, 1) if now + FLIP_LEAD < STEPS else (2, 5, 7, 0, 1)
-                        woven = 2 if now < STEPS - 1 else 1
-                        pairs = [storer(stored + i, free_banks) for i in range(woven)] + [nothing, nothing]
-                        stored = stored + woven
-                        iteration(now, (pairs[0], nothing, pairs[1], pairs[2]))
+                        works = [storer(pair, free_banks) for pair in pairs_of_turn(now)] + [nothing]
+                        iteration(now, (works[0], normaliser(now), works[1], nothing))
                     else:
                         iteration(now)
-                store_vectors(stored, (2, 5, 7, 0, 1))
+                store_vectors(FIRST_TAIL_PAIR, (2, 5, 7, 0, 1))
                 scalar_gain()
-                for pair in range(stored + 1, PAIRS):
+                for pair in range(FIRST_TAIL_PAIR + 1, PAIRS):
                     store_vectors(pair, (2, 5, 7, 0, 1))
                 all_banks = (0, 1, 2, 3, 4, 5, 6, 7)
                 normalise_scalars(0)

@@ -191,12 +191,21 @@ def tile_feedforward_pb_t_kernel(
                 by_q = x_vectors_of[c][:].rearrange("p t (q r) -> p (t q) r", r=4 * DV)
                 component = by_q.rearrange("p m (u e d) -> p d m u e", u=2, e=2, d=DV)[:, g - 1]
                 in_order = picked[:].rearrange("p u m e -> p m u e")
-                pieces = 2 if c == 0 else 1
-                width = CHUNK // pieces
-                for piece in range(pieces):
-                    nc.vector.tensor_copy(
-                        out=in_order[:, piece * width : (piece + 1) * width],
-                        in_=component[:, piece * width : (piece + 1) * width],
+                if c == 0:
+                    for first in (0, CHUNK // 2):
+                        cols = slice(first, first + CHUNK // 2)
+                        nc.vector.tensor_copy(out=in_order[:, cols], in_=component[:, cols])
+                else:
+                    cols = slice(0, 322)
+                    nc.vector.tensor_copy(out=in_order[:, cols], in_=component[:, cols])
+                    cols = slice(320, CHUNK)
+                    nc.gpsimd.tensor_scalar(
+                        out=in_order[:, cols],
+                        in0=component[:, cols],
+                        scalar1=1.0,
+                        scalar2=0.0,
+                        op0=MULT,
+                        op1=ADD,
                     )
                 picked_of[s] = picked
                 if g == DV:
@@ -221,7 +230,7 @@ def tile_feedforward_pb_t_kernel(
                     return
                 if g == 1:
                     f_cols_of[c] = bypass_in.tile([P, DV, CHUNK], BF16, name="f_cols")
-                    nc.scalar.copy(out=f_cols_scalar[:, c, :], in_=f_flipped[:, 0, :])
+                    nc.vector.tensor_copy(out=f_cols_scalar[:, c, :], in_=f_flipped[:, 0, :])
                     nc.vector.tensor_copy(out=f_cols_of[c][:, 0, :], in_=f_flipped[:, 1, :])
                 if g == DV:
                     nc.vector.tensor_copy(out=f_cols_of[c][:, 1:DV, :], in_=f_flipped[:])
@@ -243,7 +252,7 @@ def tile_feedforward_pb_t_kernel(
                         nc.tensor.transpose(flipped[:, u, t - 2 * half, :], words, ident_f32[:])
                 if half == 0:
                     grouped_of[s] = grouping.tile([P, CHUNK, 2], F32, name="grouped", align_bytes=64)
-                copy_out = nc.vector.tensor_copy if sorting_done(s) else nc.scalar.copy
+                copy_out = nc.vector.tensor_copy if sorting_done(s) or (half == 1 and 3 < s < VECTOR_STEPS and s % 4 == 0) else nc.scalar.copy
                 copy_out(
                     out=grouped_of[s][:, half * 2 * P : (half + 1) * 2 * P, :],
                     in_=flipped[:].rearrange("p u i n -> p (i n) u"),
@@ -329,13 +338,13 @@ def tile_feedforward_pb_t_kernel(
                 return
 
             def iteration(now, between=(nothing, nothing, nothing, nothing)):
+                run(quantise_step, now + FLIP_LEAD - 1)
                 run(sort_step, now + SORT_LEAD)
                 run(flip_half, now + FLIP_LEAD, 0)
                 run(multiply_half, now, 0)
                 run(bypass_half, now + 1, 0)
                 between[0]()
                 run(flip_half, now + FLIP_LEAD, 1)
-                run(quantise_step, now + FLIP_LEAD - 1)
                 run(add_half, now, 0)
                 between[1]()
                 run(multiply_half, now, 1)

@@ -196,9 +196,9 @@ def tile_feedforward_pb_t_kernel(
                         cols = slice(first, first + CHUNK // 2)
                         nc.vector.tensor_copy(out=in_order[:, cols], in_=component[:, cols])
                 else:
-                    cols = slice(0, 322)
+                    cols = slice(0, 258)
                     nc.vector.tensor_copy(out=in_order[:, cols], in_=component[:, cols])
-                    cols = slice(320, CHUNK)
+                    cols = slice(256, CHUNK)
                     nc.gpsimd.tensor_scalar(
                         out=in_order[:, cols],
                         in0=component[:, cols],
@@ -237,7 +237,7 @@ def tile_feedforward_pb_t_kernel(
                     load_features(c + 2)
 
             def sorting_done(s):
-                return VECTOR_STEPS - SORT_LEAD <= s - FLIP_LEAD < VECTOR_STEPS
+                return VECTOR_STEPS - SORT_LEAD <= s - FLIP_LEAD < VECTOR_STEPS + 1
 
             def flip_half(s, half):
                 c, g = place(s)
@@ -252,7 +252,7 @@ def tile_feedforward_pb_t_kernel(
                         nc.tensor.transpose(flipped[:, u, t - 2 * half, :], words, ident_f32[:])
                 if half == 0:
                     grouped_of[s] = grouping.tile([P, CHUNK, 2], F32, name="grouped", align_bytes=64)
-                copy_out = nc.vector.tensor_copy if sorting_done(s) or (half == 1 and 3 < s < VECTOR_STEPS and s % 4 == 0) else nc.scalar.copy
+                copy_out = nc.vector.tensor_copy if sorting_done(s) or (half == 1 and 3 < s < VECTOR_STEPS and s % 3 == 0) else nc.scalar.copy
                 copy_out(
                     out=grouped_of[s][:, half * 2 * P : (half + 1) * 2 * P, :],
                     in_=flipped[:].rearrange("p u i n -> p (i n) u"),
@@ -338,7 +338,8 @@ def tile_feedforward_pb_t_kernel(
                 return
 
             def iteration(now, between=(nothing, nothing, nothing, nothing)):
-                run(quantise_step, now + FLIP_LEAD - 1)
+                if now != VECTOR_STEPS + 1:
+                    run(quantise_step, now + FLIP_LEAD - 1)
                 run(sort_step, now + SORT_LEAD)
                 run(flip_half, now + FLIP_LEAD, 0)
                 run(multiply_half, now, 0)
@@ -403,6 +404,7 @@ def tile_feedforward_pb_t_kernel(
                 )
 
             def vector_gain():
+                quantise_step(VECTOR_STEPS + FLIP_LEAD)
                 nc.vector.reciprocal(out=gain[:, HALVES:], in_=spread[:, HALVES:])
                 nc.vector.tensor_mul(
                     out=gain[:, HALVES:], in0=gain[:, HALVES:], in1=norm_cols[:, HALVES : 2 * HALVES]

@@ -35,13 +35,13 @@ PAUSE = 1
 STEPS = VECTOR_STEPS + PAUSE + CHUNKS
 LAST_VECTOR_STEP = VECTOR_STEPS - 1
 FLIP_LEAD = 3
-SORT_LEAD = FLIP_LEAD + 1
+SORT_LEAD = FLIP_LEAD + 2
 FIRST_STORE = VECTOR_STEPS + 2
 LAST_VECTOR_INPUT = VECTOR_STEPS - FLIP_LEAD
 LATE = 1
 EARLY = 1 - LATE
 PAIRS = NODE_TILES // 2
-SCALARS_AHEAD = 4
+SCALARS_AHEAD = 3
 TAIL_PAIRS = 2
 FIRST_TAIL_PAIR = PAIRS - TAIL_PAIRS
 EPS = 1e-5
@@ -114,7 +114,7 @@ def tile_feedforward_pb_t_kernel(
 
         with ExitStack() as vector_input:
             loads = vector_input.enter_context(tc.tile_pool(name="loads", bufs=2))
-            sorting = vector_input.enter_context(tc.tile_pool(name="sorting", bufs=2))
+            sorting = vector_input.enter_context(tc.tile_pool(name="sorting", bufs=3))
 
             def load_vectors(c):
                 if c >= CHUNKS:
@@ -174,8 +174,6 @@ def tile_feedforward_pb_t_kernel(
             load_features(1)
             load_weights(0)
             nc.sync.dma_start(out=byp_w[:, 0, :], in_=byp_W0)
-            for c in range(SCALARS_AHEAD):
-                load_scalars(c)
 
             norm_rows = keep.tile([P, P], BF16)
             nc.vector.memset(norm_rows[:], 0.0)
@@ -196,9 +194,9 @@ def tile_feedforward_pb_t_kernel(
                         cols = slice(first, first + CHUNK // 2)
                         nc.vector.tensor_copy(out=in_order[:, cols], in_=component[:, cols])
                 else:
-                    cols = slice(0, 258)
+                    cols = slice(0, 194)
                     nc.vector.tensor_copy(out=in_order[:, cols], in_=component[:, cols])
-                    cols = slice(256, CHUNK)
+                    cols = slice(192, CHUNK)
                     nc.gpsimd.tensor_scalar(
                         out=in_order[:, cols],
                         in0=component[:, cols],
@@ -210,6 +208,8 @@ def tile_feedforward_pb_t_kernel(
                 picked_of[s] = picked
                 if g == DV:
                     load_vectors(c + 2)
+                    if 0 < c <= SCALARS_AHEAD:
+                        load_scalars(c - 1)
 
             def flip_features(s, half):
                 c, g = place(s)
@@ -252,7 +252,7 @@ def tile_feedforward_pb_t_kernel(
                         nc.tensor.transpose(flipped[:, u, t - 2 * half, :], words, ident_f32[:])
                 if half == 0:
                     grouped_of[s] = grouping.tile([P, CHUNK, 2], F32, name="grouped", align_bytes=64)
-                copy_out = nc.vector.tensor_copy if sorting_done(s) or (half == 1 and 3 < s < VECTOR_STEPS and s % 3 == 0) else nc.scalar.copy
+                copy_out = nc.vector.tensor_copy if sorting_done(s) or (half == 1 and 3 < s < VECTOR_STEPS and s % 2 == 0) else nc.scalar.copy
                 copy_out(
                     out=grouped_of[s][:, half * 2 * P : (half + 1) * 2 * P, :],
                     in_=flipped[:].rearrange("p u i n -> p (i n) u"),

@@ -252,7 +252,7 @@ def tile_feedforward_pb_t_kernel(
                         nc.tensor.transpose(flipped[:, u, t - 2 * half, :], words, ident_f32[:])
                 if half == 0:
                     grouped_of[s] = grouping.tile([P, CHUNK, 2], F32, name="grouped", align_bytes=64)
-                copy_out = nc.vector.tensor_copy if sorting_done(s) or (half == 1 and 3 < s < VECTOR_STEPS and s % 2 == 0) else nc.scalar.copy
+                copy_out = nc.vector.tensor_copy if (half == 1 or s % 2) and sorting_done(s) or (half == 1 and 3 < s < VECTOR_STEPS and s % 3) else nc.scalar.copy
                 copy_out(
                     out=grouped_of[s][:, half * 2 * P : (half + 1) * 2 * P, :],
                     in_=flipped[:].rearrange("p u i n -> p (i n) u"),

import math
from contextlib import ExitStack

import concourse.mybir as mybir
from concourse.masks import make_identity

F32 = mybir.dt.float32
BF16 = mybir.dt.bfloat16
I32 = mybir.dt.int32
U32 = mybir.dt.uint32
U8 = mybir.dt.uint8
FP8X4 = mybir.dt.float8_e4m3fn_x4
FP4X4 = mybir.dt.float4_e2m1fn_x4
ADD = mybir.AluOpType.add
MULT = mybir.AluOpType.mult
SUBTRACT = mybir.AluOpType.subtract
SQUARE = mybir.ActivationFunctionType.Square
SQRT = mybir.ActivationFunctionType.Sqrt

P = 128
NODES = 4096
NODE_TILES = NODES // P
CHUNK_TILES = 4
CHUNK = CHUNK_TILES * P
CHUNKS = NODES // CHUNK
DV = 3
GROUPS = 1 + DV
HID = 512
BYP = 128
OUT = 256
HALVES = OUT // P
BLOCKS = GROUPS * HALVES
VECTOR_STEPS = CHUNKS * DV
PAUSE = 1
STEPS = VECTOR_STEPS + PAUSE + CHUNKS
LAST_VECTOR_STEP = VECTOR_STEPS - 1
FLIP_LEAD = 3
SORT_LEAD = FLIP_LEAD + 2
FIRST_STORE = VECTOR_STEPS + 2
LAST_VECTOR_INPUT = VECTOR_STEPS - FLIP_LEAD
LATE = 1
EARLY = 1 - LATE
PAIRS = NODE_TILES // 2
SCALARS_AHEAD = 3
TAIL_PAIRS = 2
FIRST_TAIL_PAIR = PAIRS - TAIL_PAIRS
EPS = 1e-5

FLOPS = 2 * NODES * GROUPS * OUT * (HID + BYP)


def tile_feedforward_pb_t_kernel(
    tc,
    h2,
    features,
    lin3_W0_words,
    lin3_W0_scales,
    lin3_W1_words,
    lin3_W1_scales,
    byp_W0,
    byp_W1,
    bn_weight,
    bn_bias,
    out,
):
    nc = tc.nc
    h2_tiles = h2.rearrange("(p j) c -> p j c", j=NODE_TILES)
    features_tiles = features.rearrange("(p j) c -> p j c", j=NODE_TILES)
    out_tiles = out.rearrange("(p j) c -> p j c", j=NODE_TILES)

    with ExitStack() as whole:
        keep = whole.enter_context(tc.tile_pool(name="keep", bufs=1))
        scalar_in = whole.enter_context(tc.tile_pool(name="scalar_in", bufs=SCALARS_AHEAD))
        grouping = whole.enter_context(tc.tile_pool(name="grouping", bufs=2))
        quantised = whole.enter_context(tc.tile_pool(name="quantised", bufs=FLIP_LEAD + 1))
        bypass_in = whole.enter_context(tc.tile_pool(name="bypass_in", bufs=2))
        sums = whole.enter_context(tc.tile_pool(name="sums", bufs=5))
        scrap = whole.enter_context(tc.tile_pool(name="scrap", bufs=2))
        banks = whole.enter_context(tc.psum_pool(name="banks", bufs=1))

        def bank(index, shape, dtype):
            return banks.tile(shape, dtype, name="bank%d" % index)

        y = keep.tile([P, BLOCKS, NODES], F32)
        scalar_stats = keep.tile([P, HALVES, CHUNKS, 6], F32)
        vector_squares = keep.tile([P, HALVES, DV, CHUNKS], F32)
        gain = keep.tile([P, 2 * HALVES], F32)
        shift = keep.tile([P, HALVES], F32)
        f_cols_scalar = keep.tile([P, CHUNKS, CHUNK], BF16)

        x_vectors_of = {}
        x_scalars_of = {}
        f_rows_of = {}
        picked_of = {}
        grouped_of = {}
        f_flipped_of = {}
        f_cols_of = {}
        operand_of = {}
        product_of = {}
        bypass_of = {}

        def place(s):
            if s < VECTOR_STEPS:
                return s // DV, 1 + s % DV
            return s - VECTOR_STEPS - PAUSE, 0

        def load_scalars(c):
            if c >= CHUNKS:
                return
            tiles = slice(c * CHUNK_TILES, (c + 1) * CHUNK_TILES)
            x_scalars = scalar_in.tile([P, CHUNK_TILES, HID], BF16, name="x_scalars")
            nc.sync.dma_start(out=x_scalars[:], in_=h2_tiles[:, tiles, 0:HID])
            x_scalars_of[c] = x_scalars

        with ExitStack() as vector_input:
            loads = vector_input.enter_context(tc.tile_pool(name="loads", bufs=2))
            sorting = vector_input.enter_context(tc.tile_pool(name="sorting", bufs=3))

            def load_vectors(c):
                if c >= CHUNKS:
                    return
                tiles = slice(c * CHUNK_TILES, (c + 1) * CHUNK_TILES)
                x_vectors = loads.tile([P, CHUNK_TILES, DV * HID], BF16, name="x_vectors")
                pieces = 2 if c == 0 else 1
                width = CHUNK_TILES // pieces
                for piece in range(pieces):
                    nc.sync.dma_start(
                        out=x_vectors[:, piece * width : (piece + 1) * width, :],
                        in_=h2_tiles[:, tiles.start + piece * width : tiles.start + (piece + 1) * width, HID:],
                    )
                x_vectors_of[c] = x_vectors

            def load_features(c):
                if c >= CHUNKS:
                    return
                tiles = slice(c * CHUNK_TILES, (c + 1) * CHUNK_TILES)
                f_rows = loads.tile([P, CHUNK_TILES, GROUPS * BYP], BF16, name="f_rows")
                nc.sync.dma_start(out=f_rows[:], in_=features_tiles[:, tiles, :])
                f_rows_of[c] = f_rows

            load_vectors(0)
            load_features(0)
            byp_w = keep.tile([P, 2, OUT], BF16)
            nc.sync.dma_start(out=byp_w[:, 1, :], in_=byp_W1)
            load_vectors(1)

            ident_f32 = keep.tile([P, P], F32)
            make_identity(nc, ident_f32[:])
            ident_bf16 = keep.tile([P, P], BF16)
            make_identity(nc, ident_bf16[:])

            warm = keep.tile([P, 1], F32)
            nc.vector.memset(warm[:], 1.0)
            nc.scalar.sqrt(out=warm[:], in_=warm[:])
            eps = keep.tile([P, 1], F32)
            nc.vector.memset(eps[:], EPS)

            w_words = keep.tile([P, 2, 2 * OUT], U8, align_bytes=64)
            w_planes = keep.tile([P, 2, OUT], U8, align_bytes=64)
            nc.vector.memset(w_planes[:].rearrange("p w n -> p (w n)").bitcast(I32), 0)
            weights = ((lin3_W0_words, lin3_W0_scales), (lin3_W1_words, lin3_W1_scales))

            def load_weights(w):
                words, scales = weights[w]
                nc.sync.dma_start(out=w_words[:, w, :].bitcast(I32), in_=words[0].bitcast(I32))
                for quadrant in range(4):
                    nc.sync.dma_start(
                        out=w_planes[32 * quadrant : 32 * quadrant + 4, w, :].bitcast(I32),
                        in_=scales[0, 4 * quadrant : 4 * quadrant + 4, :].bitcast(I32),
                    )

            load_weights(1)

            load_features(1)
            load_weights(0)
            nc.sync.dma_start(out=byp_w[:, 0, :], in_=byp_W0)

            norm_rows = keep.tile([P, P], BF16)
            nc.vector.memset(norm_rows[:], 0.0)
            nc.sync.dma_start(out=norm_rows[0:4, :], in_=bn_weight.rearrange("(r c) -> r c", c=P))
            nc.sync.dma_start(out=norm_rows[4:6, :], in_=bn_bias.rearrange("(r c) -> r c", c=P))
            norm_cols = keep.tile([P, 8], F32)

            def sort_step(s):
                c, g = place(s)
                if g == 0:
                    return
                picked = sorting.tile([P, 2, CHUNK, 2], BF16, name="picked")
                by_q = x_vectors_of[c][:].rearrange("p t (q r) -> p (t q) r", r=4 * DV)
                component = by_q.rearrange("p m (u e d) -> p d m u e", u=2, e=2, d=DV)[:, g - 1]
                in_order = picked[:].rearrange("p u m e -> p m u e")
                if c == 0:
                    for first in (0, CHUNK // 2):
                        cols = slice(first, first + CHUNK // 2)
                        nc.vector.tensor_copy(out=in_order[:, cols], in_=component[:, cols])
                else:
                    cols = slice(0, 194)
                    nc.vector.tensor_copy(out=in_order[:, cols], in_=component[:, cols])
                    cols = slice(192, CHUNK)
                    nc.gpsimd.tensor_scalar(
                        out=in_order[:, cols],
                        in0=component[:, cols],
                        scalar1=1.0,
                        scalar2=0.0,
                        op0=MULT,
                        op1=ADD,
                    )
                picked_of[s] = picked
                if g == DV:
                    load_vectors(c + 2)
                    if 0 < c <= SCALARS_AHEAD:
                        load_scalars(c - 1)

            def flip_features(s, half):
                c, g = place(s)
                fill = 0 if g == 1 else 1
                if half == 0 and g != DV:
                    f_flipped_of[(c, fill)] = bank(2, [P, 2, CHUNK], BF16)
                f_flipped = f_flipped_of[(c, fill)]
                for group in ((0, 1) if g == 1 else (g,)):
                    for t in range(2 * half, 2 * half + 2):
                        if group == 0:
                            f_columns = f_rows_of[c][:, t, 0:BYP]
                        else:
                            f_columns = f_rows_of[c][:, t, BYP + group - 1 : GROUPS * BYP : DV]
                        nc.tensor.transpose(
                            f_flipped[:, group % 2, t * P : (t + 1) * P], f_columns, ident_bf16[:]
                        )
                if half == 0:
                    return
                if g == 1:
                    f_cols_of[c] = bypass_in.tile([P, DV, CHUNK], BF16, name="f_cols")
                    nc.vector.tensor_copy(out=f_cols_scalar[:, c, :], in_=f_flipped[:, 0, :])
                    nc.vector.tensor_copy(out=f_cols_of[c][:, 0, :], in_=f_flipped[:, 1, :])
                if g == DV:
                    nc.vector.tensor_copy(out=f_cols_of[c][:, 1:DV, :], in_=f_flipped[:])
                    load_features(c + 2)

            def sorting_done(s):
                return VECTOR_STEPS - SORT_LEAD <= s - FLIP_LEAD < VECTOR_STEPS + 1

            def flip_half(s, half):
                c, g = place(s)
                flipped = bank(half if s < FIRST_STORE + FLIP_LEAD else 0, [P, 2, 2, P], F32)
                for u in range(2):
                    for t in range(2 * half, 2 * half + 2):
                        if g == 0:
                            words = x_scalars_of[c][:, t, :].bitcast(F32)[:, u : HID // 2 : 2]
                        else:
                            words = picked_of[s][:, u, t * P : (t + 1) * P, :]
                            words = words.rearrange("p q e -> p (q e)").bitcast(F32)
                        nc.tensor.transpose(flipped[:, u, t - 2 * half, :], words, ident_f32[:])
                if half == 0:
                    grouped_of[s] = grouping.tile([P, CHUNK, 2], F32, name="grouped", align_bytes=64)
                copy_out = nc.vector.tensor_copy if (half == 1 or s % 2) and sorting_done(s) or (half == 1 and 3 < s < VECTOR_STEPS and s % 3) else nc.scalar.copy
                copy_out(
                    out=grouped_of[s][:, half * 2 * P : (half + 1) * 2 * P, :],
                    in_=flipped[:].rearrange("p u i n -> p (i n) u"),
                )
                if g > 0:
                    flip_features(s, half)
                elif half == 1:
                    load_scalars(c + SCALARS_AHEAD)

            def quantise_step(s):
                codes = quantised.tile([P, CHUNK], U32, name="codes", align_bytes=64)
                planes = quantised.tile([P, CHUNK], U8, name="planes", align_bytes=64)
                nc.vector.quantize_mx(
                    out=codes[:].bitcast(FP8X4),
                    scales=planes[:],
                    in_=grouped_of[s][:].rearrange("p n u -> p (n u)").bitcast(BF16),
                )
                operand_of[s] = (codes, planes)

            def multiply_half(s, h):
                c, g = place(s)
                codes, planes = operand_of[s]
                w = min(g, 1)
                mx_acc = bank(3 + (2 * s + h) % 3 if g > 0 else 3 + h, [P, CHUNK], F32)
                nc.tensor.matmul_mx(
                    out=mx_acc[:],
                    lhsT=w_words[:, w, 2 * h * P : 2 * (h + 1) * P].bitcast(FP4X4),
                    lhsT_scale=w_planes[:, w, h * P : (h + 1) * P],
                    rhs=codes[:].bitcast(FP8X4),
                    rhs_scale=planes[:],
                    start=True,
                    stop=True,
                )
                product_of[(s, h)] = mx_acc

            def bypass_half(s, h):
                c, g = place(s)
                w = min(g, 1)
                byp_acc = bank(6 + h if g > 0 else 6, [P, CHUNK], F32)
                nc.tensor.matmul(
                    byp_acc[:],
                    lhsT=byp_w[:, w, h * P : (h + 1) * P],
                    rhs=f_cols_of[c][:, g - 1, :] if g > 0 else f_cols_scalar[:, c, :],
                    start=True,
                    stop=True,
                )
                bypass = sums.tile([P, CHUNK], F32, name="bypass")
                nc.scalar.mul(out=bypass[:], in_=byp_acc[:], mul=1.0 / math.sqrt(BYP))
                bypass_of[(s, h)] = bypass

            def add_half(s, h):
                c, g = place(s)
                mx_acc, bypass = product_of[(s, h)], bypass_of[(s, h)]
                nc.vector.scalar_tensor_tensor(
                    out=y[:, 2 * g + h, c * CHUNK : (c + 1) * CHUNK],
                    in0=mx_acc[:],
                    scalar=1.0 / math.sqrt(HID),
                    in1=bypass[:],
                    op0=MULT,
                    op1=ADD,
                )

            def measure_step(s):
                c, g = place(s)
                for h in range(HALVES):
                    y_part = y[:, 2 * g + h, c * CHUNK : (c + 1) * CHUNK]
                    if g == 0:
                        nc.vector.bn_stats(out=scalar_stats[:, h, c, :], in_=y_part)
                    else:
                        squares = scrap.tile([P, CHUNK], BF16, name="squares")
                        nc.scalar.activation(
                            out=squares[:],
                            in_=y_part,
                            func=SQUARE,
                            accum_out=vector_squares[:, h, g - 1, c : c + 1],
                        )

            def run(stage, s, *part):
                if 0 <= s < VECTOR_STEPS or VECTOR_STEPS + PAUSE <= s < STEPS:
                    stage(s, *part)

            def nothing():
                return

            def iteration(now, between=(nothing, nothing, nothing, nothing)):
                if now != VECTOR_STEPS + 1:
                    run(quantise_step, now + FLIP_LEAD - 1)
                run(sort_step, now + SORT_LEAD)
                run(flip_half, now + FLIP_LEAD, 0)
                run(multiply_half, now, 0)
                run(bypass_half, now + 1, 0)
                between[0]()
                run(flip_half, now + FLIP_LEAD, 1)
                run(add_half, now, 0)
                between[1]()
                run(multiply_half, now, 1)
                run(bypass_half, now + 1, 1)
                between[2]()
                run(add_half, now, 1)
                if now - 1 < LAST_VECTOR_STEP:
                    run(measure_step, now - 1)
                if now >= VECTOR_STEPS:
                    run(measure_step, now)
                between[3]()

            with tc.manual_schedule():
                for now in range(-SORT_LEAD, LAST_VECTOR_INPUT):
                    iteration(now)

        with ExitStack() as storing:
            rows_out = storing.enter_context(tc.tile_pool(name="rows_out", bufs=7))
            gain_copies = storing.enter_context(tc.tile_pool(name="gain_copies", bufs=2))
            turn = {"bank": 0}

            def next_bank(free_banks, shape):
                turn["bank"] = turn["bank"] + 1
                return bank(free_banks[turn["bank"] % len(free_banks)], shape, F32)

            vector_sum = keep.tile([P, HALVES], F32)
            spread = keep.tile([P, 2 * HALVES], F32)
            gain_square = keep.tile([P, P], F32)
            gain_rows = keep.tile([P, P, DV], F32)
            mean_var = keep.tile([P, HALVES, 2], F32)

            def flip_norm():
                norm_flipped = bank(2, [P, P], BF16)
                nc.tensor.transpose(norm_flipped[:], norm_rows[:], ident_bf16[:])
                product_of["norm"] = norm_flipped

            def keep_norm():
                nc.vector.tensor_copy(out=norm_cols[:], in_=product_of["norm"][:, 0:8])

            def measure_last():
                measure_step(LAST_VECTOR_STEP)

            def vector_spread():
                nc.vector.tensor_reduce(
                    out=vector_sum[:],
                    in_=vector_squares[:].rearrange("p h d c -> p h (d c)"),
                    axis=mybir.AxisListType.X,
                    op=ADD,
                )
                nc.scalar.activation(
                    out=spread[:, HALVES:],
                    in_=vector_sum[:],
                    func=SQRT,
                    scale=1.0 / (DV * NODES),
                    bias=eps[:],
                )

            def vector_gain():
                quantise_step(VECTOR_STEPS + FLIP_LEAD)
                nc.vector.reciprocal(out=gain[:, HALVES:], in_=spread[:, HALVES:])
                nc.vector.tensor_mul(
                    out=gain[:, HALVES:], in0=gain[:, HALVES:], in1=norm_cols[:, HALVES : 2 * HALVES]
                )
                nc.vector.tensor_copy(
                    out=gain_square[:],
                    in_=gain[:, HALVES + LATE : HALVES + LATE + 1].to_broadcast([P, P]),
                )
                normalise_pairs((0,))

            def flip_gain():
                gain_flipped = bank(5, [P, P], F32)
                nc.tensor.transpose(gain_flipped[:], gain_square[:], ident_f32[:])
                product_of["gain"] = gain_flipped

            def spread_gain():
                nc.vector.tensor_copy(
                    out=gain_rows[:],
                    in_=product_of["gain"][:].unsqueeze(2).to_broadcast([P, P, DV]),
                )

            def normalise_pairs(pairs):
                now_gain = gain_copies.tile([P, HALVES], F32, name="now_gain")
                nc.vector.tensor_copy(out=now_gain[:], in_=gain[:, HALVES:])
                for pair in pairs:
                    normalise_pair(pair, now_gain)

            def normalise_pair(pair, now_gain):
                cols = slice(2 * pair * P, 2 * (pair + 1) * P)
                nc.gpsimd.tensor_scalar(
                    out=y[:, 2 + EARLY : BLOCKS : 2, cols],
                    in0=y[:, 2 + EARLY : BLOCKS : 2, cols],
                    scalar1=now_gain[:, EARLY : EARLY + 1],
                    scalar2=0.0,
                    op0=MULT,
                    op1=ADD,
                )
                for tile in (2 * pair, 2 * pair + 1):
                    if early_after_all(tile):
                        nc.gpsimd.tensor_scalar(
                            out=y[:, 2 + LATE : BLOCKS : 2, tile * P : (tile + 1) * P],
                            in0=y[:, 2 + LATE : BLOCKS : 2, tile * P : (tile + 1) * P],
                            scalar1=now_gain[:, LATE : LATE + 1],
                            scalar2=0.0,
                            op0=MULT,
                            op1=ADD,
                        )

            def early_after_all(tile):
                return tile % 4 == 3 or tile >= 2 * FIRST_TAIL_PAIR

            def store_vectors(pair, free_banks):
                rows = rows_out.tile([P, 2, DV * OUT], F32, name="rows")
                for i in range(2):
                    nodes = slice((2 * pair + i) * P, (2 * pair + i + 1) * P)
                    for h in (LATE, EARLY):
                        vectors_t = next_bank(free_banks, [P, DV, P])
                        for d in range(DV):
                            nc.tensor.transpose(
                                vectors_t[:, d, :], y[:, 2 * (1 + d) + h, nodes], ident_f32[:]
                            )
                        part = rows[:, i, h * DV * P : (h + 1) * DV * P].rearrange(
                            "p (o d) -> p o d", d=DV
                        )
                        if h == LATE and not early_after_all(2 * pair + i):
                            nc.vector.tensor_tensor(
                                out=part,
                                in0=vectors_t[:].rearrange("p d o -> p o d"),
                                in1=gain_rows[:],
                                op=MULT,
                            )
                        else:
                            nc.scalar.copy(out=part, in_=vectors_t[:].rearrange("p d o -> p o d"))
                nc.sync.dma_start(out=out_tiles[:, 2 * pair : 2 * pair + 2, OUT:], in_=rows[:])

            def scalar_gain():
                for h in range(HALVES):
                    nc.vector.bn_aggr(
                        out=mean_var[:, h, :], in_=scalar_stats[:, h].rearrange("p c s -> p (c s)")
                    )
                nc.scalar.activation(
                    out=spread[:, 0:HALVES], in_=mean_var[:, :, 1], func=SQRT, bias=eps[:]
                )
                nc.vector.reciprocal(out=gain[:, 0:HALVES], in_=spread[:, 0:HALVES])
                nc.vector.tensor_mul(
                    out=gain[:, 0:HALVES], in0=gain[:, 0:HALVES], in1=norm_cols[:, 0:HALVES]
                )
                for h in range(HALVES):
                    nc.vector.scalar_tensor_tensor(
                        out=shift[:, h : h + 1],
                        in0=mean_var[:, h, 0:1],
                        scalar=gain[:, h : h + 1],
                        in1=norm_cols[:, 2 * HALVES + h : 2 * HALVES + h + 1],
                        op0=MULT,
                        op1=SUBTRACT,
                    )

            def normalise_scalars(c):
                if c >= CHUNKS:
                    return
                cols = slice(c * CHUNK, (c + 1) * CHUNK)
                for h in range(HALVES):
                    nc.vector.tensor_scalar(
                        out=y[:, h, cols],
                        in0=y[:, h, cols],
                        scalar1=gain[:, h : h + 1],
                        scalar2=shift[:, h : h + 1],
                        op0=MULT,
                        op1=SUBTRACT,
                    )

            def store_scalars(c, free_banks):
                rows = rows_out.tile([P, CHUNK_TILES, OUT], F32, name="rows")
                for i in range(0, CHUNK_TILES, 2):
                    scalars_t = next_bank(free_banks, [P, 2, OUT])
                    for t in range(2):
                        nodes = slice((c * CHUNK_TILES + i + t) * P, (c * CHUNK_TILES + i + t + 1) * P)
                        for h in range(HALVES):
                            nc.tensor.transpose(
                                scalars_t[:, t, h * P : (h + 1) * P], y[:, h, nodes], ident_f32[:]
                            )
                    copy_out = nc.scalar.copy if i == 0 else nc.vector.tensor_copy
                    copy_out(out=rows[:, i : i + 2, :], in_=scalars_t[:])
                tiles = slice(c * CHUNK_TILES, (c + 1) * CHUNK_TILES)
                nc.sync.dma_start(out=out_tiles[:, tiles, 0:OUT], in_=rows[:])

            def storer(pair, free_banks):
                return lambda: store_vectors(pair, free_banks)

            def pairs_of_turn(now):
                first = max(0, 2 * (now - FIRST_STORE) + 1)
                if now == STEPS:
                    return range(FIRST_TAIL_PAIR, PAIRS)
                return range(first, min(2 * (now - FIRST_STORE) + 3, FIRST_TAIL_PAIR))

            def normalise_ahead(now):
                first = 2 * (now - FIRST_STORE) + 4 if now >= FIRST_STORE else 1
                normalise_pairs(range(first, min(2 * (now - FIRST_STORE) + 6, PAIRS)))

            def normaliser(now):
                return lambda: normalise_ahead(now)

            def spread_and_normalise():
                spread_gain()
                normalise_ahead(FIRST_STORE - 1)

            with tc.manual_schedule():
                for now in range(LAST_VECTOR_INPUT, STEPS):
                    if now == LAST_VECTOR_INPUT:
                        iteration(now, (flip_norm, nothing, keep_norm, nothing))
                    elif now == VECTOR_STEPS:
                        iteration(now, (measure_last, nothing, vector_spread, vector_gain))
                    elif now == VECTOR_STEPS + 1:
                        iteration(now, (flip_gain, spread_and_normalise, storer(0, (2, 5, 7)), nothing))
                    elif now >= FIRST_STORE:
                        free_banks = (2, 5, 7, 1) if now + FLIP_LEAD < STEPS else (2, 5, 7, 0, 1)
                        works = [storer(pair, free_banks) for pair in pairs_of_turn(now)] + [nothing]
                        iteration(now, (works[0], normaliser(now), works[1], nothing))
                    else:
                        iteration(now)
                store_vectors(FIRST_TAIL_PAIR, (2, 5, 7, 0, 1))
                scalar_gain()
                for pair in range(FIRST_TAIL_PAIR + 1, PAIRS):
                    store_vectors(pair, (2, 5, 7, 0, 1))
                all_banks = (0, 1, 2, 3, 4, 5, 6, 7)
                normalise_scalars(0)
                for c in range(CHUNKS):
                    normalise_scalars(c + 1)
                    store_scalars(c, all_banks)
